import numpy as np
import ml_dtypes


def mxq(x, axis, fmt="e4m3"):
    dtype, down = {"e4m3": (ml_dtypes.float8_e4m3fn, 7), "e5m2": (ml_dtypes.float8_e5m2, 14)}[fmt]
    v = np.moveaxis(np.asarray(x, np.float32).astype(ml_dtypes.bfloat16).astype(np.float64), axis, -1)
    blocks = v.reshape(v.shape[:-1] + (-1, 32))
    amax = np.abs(blocks).max(-1, keepdims=True)
    byte = np.maximum(np.where(amax > 0, np.frexp(amax)[1] - 1 + 127, 0) - down, 1)
    scale = np.exp2(byte - 127.0)
    codes = (blocks / scale).astype(np.float32).astype(dtype).astype(np.float64)
    return np.moveaxis((codes * scale).reshape(v.shape), -1, axis)


WIDE = False


def mx_kscale(k):
    if not WIDE:
        return np.ones(k)
    levels = np.array([18, -18])
    if k % 512:
        return np.exp2(np.random.permutation(np.resize(levels, k // 32))).repeat(32)
    a = np.empty((k // 512, 16))
    for p in range(k // 512):
        a[p, :8] = np.random.permutation(np.resize(levels, 8))
        for g in range(8):
            far = levels[np.abs(levels - a[p, g]) >= 10]
            a[p, g + 8] = far[np.random.randint(len(far))]
    return np.exp2(a.ravel()).repeat(32)


BF16 = ml_dtypes.bfloat16


def bf(x):
    return np.asarray(x, np.float32).astype(BF16)


def f64(x):
    return np.asarray(x).astype(np.float64)


B, T, C, H, D = 1, 1024, 1024, 16, 128
EPS = 1e-6
THETA = 10000.0


def rope_back(g, cos, sin):
    ge, go = g[..., 0::2], g[..., 1::2]
    c, s = cos[None, :, None, :], sin[None, :, None, :]
    return np.stack([ge * c + go * s, go * c - ge * s], axis=-1).reshape(g.shape)


def setup_inputs():
    s = mx_kscale(T)
    u = mx_kscale(H * D)[::D]
    ang = np.outer(np.arange(T), 1.0 / THETA ** (np.arange(0, D, 2) / D))
    x0 = bf(np.random.standard_normal((B, T, C)))
    w0 = bf(np.random.standard_normal((H * D, C)) / np.sqrt(C))
    q_norm_w = bf(1.0 + 0.1 * np.random.standard_normal(D))
    g = np.random.standard_normal((B, T, H, D)) * np.exp2(np.random.randint(-6, 1, (B, T, 1, 1)))
    g = bf(g / s[None, :, None, None] * u[None, None, :, None])
    q = (f64(x0) @ f64(w0).T).reshape(B, T, H, D)
    rstd = 1.0 / np.sqrt(np.mean(q * q, axis=-1) + EPS)
    return {"x": bf(f64(x0) * s[None, :, None]),
            "wq": bf(f64(w0) / np.repeat(u, D)[:, None]),
            "q_norm_w": q_norm_w,
            "freqs_cos": bf(np.cos(ang)), "freqs_sin": bf(np.sin(ang)),
            "q": np.asarray(q, np.float32), "rstd": np.asarray(rstd, np.float32),
            "grad_out": g}


def reference(x, wq, q_norm_w, freqs_cos, freqs_sin, q, rstd, grad_out):
    r = f64(rstd)[..., None]
    qh = f64(q) * r
    dh = rope_back(f64(grad_out), f64(freqs_cos), f64(freqs_sin)) * f64(q_norm_w)
    dq = r * (dh - qh * np.mean(dh * qh, axis=-1, keepdims=True))
    dq = dq.reshape(B * T, H * D)
    xf = f64(x).reshape(B * T, C)
    dx = mxq(dq, 1, "e5m2") @ mxq(f64(wq), 0, "e4m3")
    dwq = mxq(dq, 0, "e5m2").T @ mxq(xf, 0, "e4m3")
    return dx.reshape(B, T, C), dwq

@@ -1,0 +1,353 @@
+from contextlib import ExitStack
+
+import concourse.mybir as mybir
+from concourse.masks import make_identity
+
+F32 = mybir.dt.float32
+BF16 = mybir.dt.bfloat16
+U32 = mybir.dt.uint32
+U8 = mybir.dt.uint8
+E4M3 = mybir.dt.float8_e4m3fn_x4
+E5M2 = mybir.dt.float8_e5m2_x4
+ALU = mybir.AluOpType
+ACTF = mybir.ActivationFunctionType
+
+T, C, H, D = 1024, 1024, 16, 128
+FLOPS = 2 * 2 * T * C * H * D
+P = 128
+NG = 4
+NS = 32
+
+
+def tile_mla_pb_v_kernel(tc, x, wq, q_norm_w, freqs_cos, freqs_sin, q, rstd, grad_out, out_0, out_1):
+    nc = tc.nc
+    qf = q.rearrange("b t n d -> (b t) (n d)")
+    gf = grad_out.rearrange("b t n d -> (b t) (n d)")
+    xf = x.rearrange("b t c -> (b t) c")
+    rf = rstd.rearrange("b t n -> (b t) n")
+    of = out_0.rearrange("b t c -> (b t) c")
+
+    with ExitStack() as ctx:
+        const = ctx.enter_context(tc.tile_pool(name="const", bufs=1))
+        loads = ctx.enter_context(tc.tile_pool(name="loads", bufs=3))
+        work = ctx.enter_context(tc.tile_pool(name="work", bufs=2))
+        psum = ctx.enter_context(tc.psum_pool(name="psum", bufs=1))
+        ctx.enter_context(tc.manual_schedule())
+
+        wrow = const.tile([P, D], BF16, name="wrow")
+        nc.sync.dma_start(out=wrow[:], in_=q_norm_w.partition_broadcast(P))
+        cosr = const.tile([P, 2, 4, 64], BF16, name="cosr")
+        sinr = const.tile([P, 2, 4, 64], BF16, name="sinr")
+        nc.sync.dma_start(out=cosr[:], in_=freqs_cos.rearrange("(h p j) d -> p h j d", h=2, j=4))
+        nc.sync.dma_start(out=sinr[:], in_=freqs_sin.rearrange("(h p j) d -> p h j d", h=2, j=4))
+
+        g_tiles = {}
+        q_tiles = {}
+
+        def load(u):
+            G, h = divmod(u, 2)
+            gt = loads.tile([P, 4, 512], BF16, name="gt")
+            qt = loads.tile([P, 4, 512], F32, name="qt")
+            rows = slice(512 * h, 512 * h + 512)
+            cols = slice(512 * G, 512 * G + 512)
+            nc.sync.dma_start(out=gt[:], in_=gf[rows, cols].rearrange("(p j) w -> p j w", j=4))
+            nc.sync.dma_start(out=qt[:], in_=qf[rows, cols].rearrange("(p j) w -> p j w", j=4))
+            g_tiles[u] = gt
+            q_tiles[u] = qt
+
+        raw_tiles = {}
+
+        def load_raw(key, ap):
+            rt = loads.tile([P, 4, 1024], BF16, name="raw", bufs=2)
+            nc.sync.dma_start(out=rt[:], in_=ap.rearrange("(p j) c -> p j c", j=4))
+            raw_tiles[key] = rt
+
+        load(0)
+        rst = const.tile([P, 2, 4, H], F32, name="rst")
+        nc.sync.dma_start(out=rst[:], in_=rf.rearrange("(h p j) n -> p h j n", h=2, j=4))
+        load(1)
+
+        ident = const.tile([P, P], F32, name="ident")
+        make_identity(nc, ident[:])
+        identb = const.tile([P, P], BF16, name="identb")
+        nc.gpsimd.tensor_copy(out=identb[:], in_=ident[:])
+        swap = const.tile([P, 64, 2], F32, name="swap")
+        idv = ident[:].rearrange("p (a e) -> p a e", e=2)
+        nc.gpsimd.tensor_copy(out=swap[:, :, 0], in_=idv[:, :, 1])
+        nc.gpsimd.tensor_copy(out=swap[:, :, 1], in_=idv[:, :, 0])
+        swapf = swap[:].rearrange("p a e -> p (a e)")
+
+        wsrow = const.tile([P, 64, 2], BF16, name="wsrow")
+        wv = wrow[:].rearrange("p (a e) -> p a e", e=2)
+        nc.vector.tensor_scalar(out=wsrow[:, :, 0], in0=wv[:, :, 1], scalar1=-1.0, scalar2=None, op0=ALU.mult)
+        nc.vector.tensor_copy(out=wsrow[:, :, 1], in_=wv[:, :, 0])
+
+        tab = const.tile([P, 2, 2, 4, P], F32, name="tab")
+
+        def tables(h):
+            for k in range(2):
+                src = (cosr, sinr)[k]
+                gain = (wv, wsrow[:])[k]
+                tok = work.tile([P, 4, 64, 2], F32, name="tok")
+                nc.vector.tensor_tensor(
+                    out=tok[:],
+                    in0=src[:, h, :, :].unsqueeze(3).to_broadcast([P, 4, 64, 2]),
+                    in1=gain.unsqueeze(1).to_broadcast([P, 4, 64, 2]),
+                    op=ALU.mult,
+                )
+                pt = psum.tile([P, 4, P], F32, name="pt", tag="dh", bufs=3)
+                for jj in range(4):
+                    nc.tensor.transpose(pt[:, jj, :], tok[:, jj, :, :].rearrange("p a e -> p (a e)"), ident[:])
+                nc.scalar.copy(out=tab[:, k, h, :, :], in_=pt[:])
+
+        r3 = const.tile([P, 2 * 4 * H], F32, name="r3")
+        r2 = const.tile([P, 2 * 4 * H], F32, name="r2")
+        rflat = rst[:].rearrange("p h j n -> p (h j n)")
+
+        tables(0)
+        nc.vector.tensor_tensor(out=r2[:], in0=rflat, in1=rflat, op=ALU.mult)
+        nc.vector.scalar_tensor_tensor(out=r3[:], in0=r2[:], scalar=-1.0 / D, in1=rflat, op0=ALU.mult, op1=ALU.mult)
+        tables(1)
+
+        x_codes = [const.tile([P, C], U32, name="xc%d" % h, align_bytes=64) for h in range(2)]
+        x_scales = [const.tile([P, C], U8, name="xs%d" % h, align_bytes=64) for h in range(2)]
+        w_codes = [const.tile([P, C], U32, name="wc%d" % G, align_bytes=64) for G in range(NG)]
+        w_scales = [const.tile([P, C], U8, name="ws%d" % G, align_bytes=64) for G in range(NG)]
+        f_codes = [const.tile([P, T], U32, name="fc%d" % G, align_bytes=64) for G in range(NG)]
+        f_scales = [const.tile([P, T], U8, name="fs%d" % G, align_bytes=64) for G in range(NG)]
+        t_codes = {}
+        t_scales = {}
+
+        gT = {}
+        ab = {}
+        dh = {}
+        prod = {}
+        kcol = {}
+        kq = {}
+        dq = {}
+        xin = {}
+        tin = {}
+
+        def where(s):
+            u, jj = divmod(s, 4)
+            G, h = divmod(u, 2)
+            return u, jj, G, h
+
+        def t1(s):
+            u, jj, G, h = where(s)
+            pt = psum.tile([P, 4, P], BF16, name="gT", tag="gT", bufs=2)
+            for a in range(4):
+                nc.tensor.transpose(pt[:, a, :], g_tiles[u][:, jj, a * P : (a + 1) * P], identb[:])
+            gT[s] = pt
+
+        def mul_ab(s):
+            u, jj, G, h = where(s)
+            t = work.tile([P, 2, 4, P], F32, name="ab")
+            for k in range(2):
+                nc.vector.tensor_tensor(
+                    out=t[:, k, :, :],
+                    in0=gT[s][:],
+                    in1=tab[:, k, h, jj, :].unsqueeze(1).to_broadcast([P, 4, P]),
+                    op=ALU.mult,
+                )
+            ab[s] = t
+
+        def t2(s):
+            pt = psum.tile([P, 4, P], F32, name="dh", tag="dh", bufs=3)
+            for a in range(4):
+                nc.tensor.matmul(pt[:, a, :], lhsT=ab[s][:, 0, a, :], rhs=ident[:], is_transpose=True, start=True, stop=False)
+                nc.tensor.matmul(pt[:, a, :], lhsT=ab[s][:, 1, a, :], rhs=swapf, is_transpose=True, start=False, stop=True)
+            dh[s] = pt
+
+        def mul_d(s):
+            u, jj, G, h = where(s)
+            t = work.tile([P, 4, P], F32, name="prod")
+            nc.vector.tensor_tensor(out=t[:], in0=dh[s][:], in1=q_tiles[u][:, jj, :].rearrange("p (a d) -> p a d", a=4), op=ALU.mult)
+            prod[s] = t
+
+        def red(s):
+            u, jj, G, h = where(s)
+            t = work.tile([P, 4], F32, name="kcol", bufs=3)
+            for a in range(4):
+                col = (h * 4 + jj) * H + 4 * G + a
+                junk = work.tile([P, P], BF16, name="junk")
+                nc.scalar.activation(
+                    out=junk[:], in_=prod[s][:, a, :], func=ACTF.Copy, scale=r3[:, col : col + 1], accum_out=t[:, a : a + 1]
+                )
+            kcol[s] = t
+
+        def mul_kq(s):
+            u, jj, G, h = where(s)
+            t = work.tile([P, 4, P], F32, name="kq", bufs=3)
+            for a in range(4):
+                nc.gpsimd.tensor_scalar(
+                    out=t[:, a, :],
+                    in0=q_tiles[u][:, jj, a * P : (a + 1) * P],
+                    scalar1=kcol[s][:, a : a + 1],
+                    scalar2=0.0,
+                    op0=ALU.mult,
+                    op1=ALU.add,
+                )
+            kq[s] = t
+
+        def fin(s):
+            u, jj, G, h = where(s)
+            if jj == 0:
+                dq[u] = work.tile([P, 4, 512], BF16, name="dq", bufs=3, align_bytes=64)
+            for a in range(4):
+                nc.vector.scalar_tensor_tensor(
+                    out=dq[u][:, jj, a * P : (a + 1) * P],
+                    in0=dh[s][:, a, :],
+                    scalar=rst[:, h, jj, 4 * G + a : 4 * G + a + 1],
+                    in1=kq[s][:, a, :],
+                    op0=ALU.mult,
+                    op1=ALU.add,
+                )
+
+        def t3(u, half):
+            if half == 0:
+                xin[u] = work.tile([P, 4 * P * 4], BF16, name="xin", align_bytes=64)
+            words = dq[u][:].rearrange("p j f -> p (j f)").bitcast(F32)
+            pt = psum.tile([P, 2, 2, P], F32, name="xt", tag="xt", bufs=1)
+            for a in range(2):
+                jj = 2 * half + a
+                for v in range(2):
+                    nc.tensor.transpose(pt[:, a, v, :], words[:, jj * 256 + v : (jj + 1) * 256 : 2], ident[:])
+            dst = xin[u][:, half * 1024 : (half + 1) * 1024].bitcast(F32)
+            nc.scalar.copy(out=dst.rearrange("p (a r v) -> p a r v", a=2, v=2), in_=pt[:].rearrange("p a v r -> p a r v"))
+
+        def x1(u, a):
+            if a == 0:
+                tin[u] = work.tile([P, 512, 4], BF16, name="tin", align_bytes=64)
+            nc.gpsimd.tensor_scalar(
+                out=tin[u][:, a * P : (a + 1) * P, :],
+                in0=dq[u][:, :, a * P : (a + 1) * P].rearrange("p j f -> p f j"),
+                scalar1=1.0,
+                scalar2=0.0,
+                op0=ALU.mult,
+                op1=ALU.add,
+            )
+
+        def quant_f(u):
+            G, h = divmod(u, 2)
+            cols = slice(512 * h, 512 * h + 512)
+            nc.vector.quantize_mx(out=f_codes[G][:, cols].bitcast(E5M2), scales=f_scales[G][:, cols], in_=xin[u][:])
+
+        def quant_t(u):
+            tcod = work.tile([P, 512], U32, name="tcod", bufs=4, align_bytes=64)
+            tsca = work.tile([P, 512], U8, name="tsca", bufs=4, align_bytes=64)
+            nc.vector.quantize_mx(out=tcod[:].bitcast(E5M2), scales=tsca[:], in_=tin[u][:].rearrange("p f j -> p (f j)"))
+            t_codes[u] = tcod
+            t_scales[u] = tsca
+
+        mixed = {}
+
+        def mix(key, n):
+            t = work.tile([P, 512, 4], BF16, name="mixed", align_bytes=64)
+            nc.scalar.copy(out=t[:], in_=raw_tiles[key][:, :, n * 512 : (n + 1) * 512].rearrange("p j c -> p c j"))
+            mixed[key, n] = t
+
+        def quant_w(key, n):
+            kind, i = key
+            codes = (x_codes if kind == "x" else w_codes)[i]
+            scales = (x_scales if kind == "x" else w_scales)[i]
+            cols = slice(n * 512, (n + 1) * 512)
+            nc.vector.quantize_mx(
+                out=codes[:, cols].bitcast(E4M3), scales=scales[:, cols], in_=mixed[key, n][:].rearrange("p c j -> p (c j)")
+            )
+
+        stage = {}
+
+        def mx_group(lhs, rhs, n, key, store, engine):
+            acc = psum.tile([P, 512], F32, name="acc", tag="mx", bufs=2)
+            k = len(lhs)
+            for i in range(k):
+                (lc, ls, l0), (rc, rs) = lhs[i], rhs[i]
+                nc.tensor.matmul_mx(
+                    out=acc[:],
+                    lhsT=lc[:, l0 : l0 + P].bitcast(E5M2),
+                    lhsT_scale=ls[:, l0 : l0 + P],
+                    rhs=rc[:, n * 512 : (n + 1) * 512].bitcast(E4M3),
+                    rhs_scale=rs[:, n * 512 : (n + 1) * 512],
+                    start=(i == 0),
+                    stop=(i == k - 1),
+                )
+            if n == 0:
+                stage[key] = work.tile([P, C], F32, name="ostage", bufs=3)
+            dst = stage[key][:, n * 512 : (n + 1) * 512]
+            if engine == 0:
+                nc.scalar.copy(out=dst, in_=acc[:])
+            else:
+                nc.vector.tensor_copy(out=dst, in_=acc[:])
+            if n == 1:
+                nc.sync.dma_start(out=store, in_=stage[key][:])
+
+        def dw_group(G, a, n, engine=0):
+            lhs = [(t_codes[2 * G + h], t_scales[2 * G + h], a * P) for h in range(2)]
+            rhs = [(x_codes[h], x_scales[h]) for h in range(2)]
+            r0 = (4 * G + a) * P
+            mx_group(lhs, rhs, n, ("w", G, a), out_1[r0 : r0 + P, :], engine)
+
+        def dx_group(h, jj, n, engine=0):
+            lhs = [(f_codes[G], f_scales[G], h * 512 + jj * P) for G in range(NG)]
+            rhs = [(w_codes[G], w_scales[G]) for G in range(NG)]
+            rows = of[512 * h : 512 * h + 512, :].rearrange("(p j) c -> p j c", j=4)
+            mx_group(lhs, rhs, n, ("x", h, jj), rows[:, jj, :], engine)
+
+        load_at = {0: [("x", 0)], 1: [("x", 1)], 2: [2], 5: [("w", 0)], 6: [3], 7: [("w", 1)], 9: [("w", 2)], 10: [4], 11: [("w", 3)], 14: [5], 18: [6], 22: [7]}
+        mix_at = {}
+        for i, (key, n) in enumerate([(("x", h), n) for h in range(2) for n in range(2)] + [(("w", G), n) for G in range(NG) for n in range(2)]):
+            mix_at[3 + i] = (key, n)
+        mx_queue = []
+        step = 0
+        while step < NS + 12 or mx_queue:
+            i = step
+            for item in load_at.get(i, []):
+                if isinstance(item, int):
+                    load(item)
+                else:
+                    src = xf if item[0] == "x" else wq
+                    load_raw(item, src[512 * item[1] : 512 * item[1] + 512, :])
+            if 0 <= i - 2 < NS:
+                t2(i - 2)
+            if i < NS:
+                t1(i)
+            if 0 <= i - 3 < NS:
+                mul_d(i - 3)
+                red(i - 3)
+                mul_kq(i - 3)
+            if 0 <= i - 1 < NS:
+                mul_ab(i - 1)
+            if 0 <= i - 4 < NS:
+                fin(i - 4)
+            for u in range(8):
+                if i == 4 * u + 6:
+                    t3(u, 0)
+                if i == 4 * u + 8:
+                    t3(u, 1)
+                    x1(u, 0)
+                    x1(u, 1)
+                if i == 4 * u + 9:
+                    x1(u, 2)
+                    x1(u, 3)
+                    quant_f(u)
+                if i == 4 * u + 10:
+                    quant_t(u)
+                    if u % 2 == 1:
+                        mx_queue += [("w", u // 2, a, n) for a in range(4) for n in range(2)]
+                    if u >= 6:
+                        mx_queue += [("x", u - 6, jj, n) for jj in range(4) for n in range(2)]
+            if i in mix_at:
+                mix(*mix_at[i])
+            if i - 1 in mix_at:
+                quant_w(*mix_at[i - 1])
+            tail = i > NS + 4
+            for b in range(4 if tail else 2):
+                if mx_queue:
+                    kind, i0, i1, n = mx_queue.pop(0)
+                    engine = n if tail else 0
+                    if kind == "w":
+                        dw_group(i0, i1, n, engine)
+                    else:
+                        dx_group(i0, i1, n, engine)
+            step += 1

@@ -17,10 +17,12 @@ FLOPS = 2 * 2 * T * C * H * D
 P = 128
 NG = 4
 NS = 32
+CFG = {'ord': [(0, 0), (0, 1), (1, 0), (1, 1), (2, 0), (3, 0), (2, 1), (3, 1)], 'bud': 4, 'kx': ['x0', 'x1', 'w0', 'w1', 'w2', 'w3'], 'tb1': 3, 'hb': 0, 'gsb': 2, 'abb': 3, 'gc': 0, 'bp': 1, 'ab': 1, 't2': 2, 'd': 3, 'red': 3, 'kq': 3, 'fin': 4, 'order': 't1 gc bp t2 d red ab kq fin', 'kqe': 'A', 'mixe': 'G', 'gTb': 1, 'dhb': 3, 'xtb': 1, 'mxb': 3, 'mix0': 2, 'mixn': 512, 'qw': 2, 'perstep': 2, 'xl': 1, 'gbuf': 3, 'kqb': 4, 'mixwait': 1, 'x1per': 1, 't3a': 1, 'qf': 2, 'tb': 6, 'ls': '0:x0 1:x1 2:2 5:w0 6:3 8:w1 10:4 11:w2 14:5 15:w3 18:6 22:7', 'mx': '2 4 6 8 10 12 14 16 18 20 22 24', 'me': 'GAGAGAGAGAGA', 'tw': 2, 'mixb': 2}
 
 
 def tile_mla_pb_v_kernel(tc, x, wq, q_norm_w, freqs_cos, freqs_sin, q, rstd, grad_out, out_0, out_1):
     nc = tc.nc
+    ORD = CFG["ord"]
     qf = q.rearrange("b t n d -> (b t) (n d)")
     gf = grad_out.rearrange("b t n d -> (b t) (n d)")
     xf = x.rearrange("b t c -> (b t) c")
@@ -45,7 +47,7 @@ def tile_mla_pb_v_kernel(tc, x, wq, q_norm_w, freqs_cos, freqs_sin, q, rstd, gra
         q_tiles = {}
 
         def load(u):
-            G, h = divmod(u, 2)
+            G, h = ORD[u]
             gt = loads.tile([P, 4, 512], BF16, name="gt")
             qt = loads.tile([P, 4, 512], F32, name="qt")
             rows = slice(512 * h, 512 * h + 512)
@@ -62,9 +64,9 @@ def tile_mla_pb_v_kernel(tc, x, wq, q_norm_w, freqs_cos, freqs_sin, q, rstd, gra
             nc.sync.dma_start(out=rt[:], in_=ap.rearrange("(p j) c -> p j c", j=4))
             raw_tiles[key] = rt
 
-        load(0)
         rst = const.tile([P, 2, 4, H], F32, name="rst")
         nc.sync.dma_start(out=rst[:], in_=rf.rearrange("(h p j) n -> p h j n", h=2, j=4))
+        load(0)
         load(1)
 
         ident = const.tile([P, P], F32, name="ident")
@@ -95,7 +97,7 @@ def tile_mla_pb_v_kernel(tc, x, wq, q_norm_w, freqs_cos, freqs_sin, q, rstd, gra
                     in1=gain.unsqueeze(1).to_broadcast([P, 4, 64, 2]),
                     op=ALU.mult,
                 )
-                pt = psum.tile([P, 4, P], F32, name="pt", tag="dh", bufs=3)
+                pt = psum.tile([P, 4, P], F32, name="pt", tag="dh", bufs=CFG["dhb"])
                 for jj in range(4):
                     nc.tensor.transpose(pt[:, jj, :], tok[:, jj, :, :].rearrange("p a e -> p (a e)"), ident[:])
                 nc.scalar.copy(out=tab[:, k, h, :, :], in_=pt[:])
@@ -104,10 +106,11 @@ def tile_mla_pb_v_kernel(tc, x, wq, q_norm_w, freqs_cos, freqs_sin, q, rstd, gra
         r2 = const.tile([P, 2 * 4 * H], F32, name="r2")
         rflat = rst[:].rearrange("p h j n -> p (h j n)")
 
+        def cube():
+            nc.vector.tensor_tensor(out=r2[:], in0=rflat, in1=rflat, op=ALU.mult)
+            nc.vector.scalar_tensor_tensor(out=r3[:], in0=r2[:], scalar=-1.0 / D, in1=rflat, op0=ALU.mult, op1=ALU.mult)
+
         tables(0)
-        nc.vector.tensor_tensor(out=r2[:], in0=rflat, in1=rflat, op=ALU.mult)
-        nc.vector.scalar_tensor_tensor(out=r3[:], in0=r2[:], scalar=-1.0 / D, in1=rflat, op0=ALU.mult, op1=ALU.mult)
-        tables(1)
 
         x_codes = [const.tile([P, C], U32, name="xc%d" % h, align_bytes=64) for h in range(2)]
         x_scales = [const.tile([P, C], U8, name="xs%d" % h, align_bytes=64) for h in range(2)]
@@ -130,30 +133,49 @@ def tile_mla_pb_v_kernel(tc, x, wq, q_norm_w, freqs_cos, freqs_sin, q, rstd, gra
 
         def where(s):
             u, jj = divmod(s, 4)
-            G, h = divmod(u, 2)
+            G, h = ORD[u]
             return u, jj, G, h
 
         def t1(s):
             u, jj, G, h = where(s)
-            pt = psum.tile([P, 4, P], BF16, name="gT", tag="gT", bufs=2)
+            pt = psum.tile([P, 4, P], BF16, name="gT", tag="gT", bufs=CFG["gTb"])
             for a in range(4):
                 nc.tensor.transpose(pt[:, a, :], g_tiles[u][:, jj, a * P : (a + 1) * P], identb[:])
             gT[s] = pt
 
-        def mul_ab(s):
+        HB = CFG["hb"]
+        gs = {}
+
+        def gcopy(s):
+            if HB:
+                t = work.tile([P, HB, P], BF16, name="gs", bufs=CFG["gsb"])
+                nc.scalar.copy(out=t[:], in_=gT[s][:, 4 - HB :, :])
+                gs[s] = t
+
+        def mul_b(s):
             u, jj, G, h = where(s)
-            t = work.tile([P, 2, 4, P], F32, name="ab")
-            for k in range(2):
-                nc.vector.tensor_tensor(
-                    out=t[:, k, :, :],
-                    in0=gT[s][:],
-                    in1=tab[:, k, h, jj, :].unsqueeze(1).to_broadcast([P, 4, P]),
+            ab[s] = work.tile([P, 2, 4, P], F32, name="ab", bufs=CFG["abb"])
+            if HB:
+                nc.gpsimd.tensor_tensor(
+                    out=ab[s][:, 1, 4 - HB :, :],
+                    in0=gs[s][:],
+                    in1=tab[:, 1, h, jj, :].unsqueeze(1).to_broadcast([P, HB, P]),
                     op=ALU.mult,
                 )
-            ab[s] = t
+
+        def mul_ab(s):
+            u, jj, G, h = where(s)
+            for k in range(2):
+                hh = 4 - HB * k
+                nc.vector.tensor_tensor(
+                    out=ab[s][:, k, 0:hh, :],
+                    in0=gT[s][:, 0:hh, :],
+                    in1=tab[:, k, h, jj, :].unsqueeze(1).to_broadcast([P, hh, P]),
+                    op=ALU.mult,
+                )
 
         def t2(s):
-            pt = psum.tile([P, 4, P], F32, name="dh", tag="dh", bufs=3)
+            pt = psum.tile([P, 4, P], F32, name="dh", tag="dh", bufs=CFG["dhb"])
             for a in range(4):
                 nc.tensor.matmul(pt[:, a, :], lhsT=ab[s][:, 0, a, :], rhs=ident[:], is_transpose=True, start=True, stop=False)
                 nc.tensor.matmul(pt[:, a, :], lhsT=ab[s][:, 1, a, :], rhs=swapf, is_transpose=True, start=False, stop=True)
@@ -161,33 +183,30 @@ def tile_mla_pb_v_kernel(tc, x, wq, q_norm_w, freqs_cos, freqs_sin, q, rstd, gra
 
         def mul_d(s):
             u, jj, G, h = where(s)
-            t = work.tile([P, 4, P], F32, name="prod")
+            t = work.tile([P, 4, P], F32, name="prod", bufs=3)
             nc.vector.tensor_tensor(out=t[:], in0=dh[s][:], in1=q_tiles[u][:, jj, :].rearrange("p (a d) -> p a d", a=4), op=ALU.mult)
             prod[s] = t
 
         def red(s):
             u, jj, G, h = where(s)
-            t = work.tile([P, 4], F32, name="kcol", bufs=3)
+            t = work.tile([P, 4], F32, name="kcol", bufs=4)
+            junk = work.tile([P, 4, P], BF16, name="junk", bufs=3)
             for a in range(4):
                 col = (h * 4 + jj) * H + 4 * G + a
-                junk = work.tile([P, P], BF16, name="junk")
                 nc.scalar.activation(
-                    out=junk[:], in_=prod[s][:, a, :], func=ACTF.Copy, scale=r3[:, col : col + 1], accum_out=t[:, a : a + 1]
+                    out=junk[:, a, :], in_=prod[s][:, a, :], func=ACTF.Copy, scale=r3[:, col : col + 1], accum_out=t[:, a : a + 1]
                 )
             kcol[s] = t
 
         def mul_kq(s):
             u, jj, G, h = where(s)
-            t = work.tile([P, 4, P], F32, name="kq", bufs=3)
+            t = work.tile([P, 4, P], F32, name="kq", bufs=CFG["kqb"])
             for a in range(4):
-                nc.gpsimd.tensor_scalar(
-                    out=t[:, a, :],
-                    in0=q_tiles[u][:, jj, a * P : (a + 1) * P],
-                    scalar1=kcol[s][:, a : a + 1],
-                    scalar2=0.0,
-                    op0=ALU.mult,
-                    op1=ALU.add,
-                )
+                src = q_tiles[u][:, jj, a * P : (a + 1) * P]
+                if CFG["kqe"] == "A":
+                    nc.scalar.activation(out=t[:, a, :], in_=src, func=ACTF.Copy, scale=kcol[s][:, a : a + 1])
+                else:
+                    nc.gpsimd.tensor_scalar(out=t[:, a, :], in0=src, scalar1=kcol[s][:, a : a + 1], scalar2=0.0, op0=ALU.mult, op1=ALU.add)
             kq[s] = t
 
         def fin(s):
@@ -208,7 +227,7 @@ def tile_mla_pb_v_kernel(tc, x, wq, q_norm_w, freqs_cos, freqs_sin, q, rstd, gra
             if half == 0:
                 xin[u] = work.tile([P, 4 * P * 4], BF16, name="xin", align_bytes=64)
             words = dq[u][:].rearrange("p j f -> p (j f)").bitcast(F32)
-            pt = psum.tile([P, 2, 2, P], F32, name="xt", tag="xt", bufs=1)
+            pt = psum.tile([P, 2, 2, P], F32, name="xt", tag="xt", bufs=CFG["xtb"])
             for a in range(2):
                 jj = 2 * half + a
                 for v in range(2):
@@ -216,42 +235,49 @@ def tile_mla_pb_v_kernel(tc, x, wq, q_norm_w, freqs_cos, freqs_sin, q, rstd, gra
             dst = xin[u][:, half * 1024 : (half + 1) * 1024].bitcast(F32)
             nc.scalar.copy(out=dst.rearrange("p (a r v) -> p a r v", a=2, v=2), in_=pt[:].rearrange("p a v r -> p a r v"))
 
-        def x1(u, a):
+        def interleave(out, in_, engine):
+            if engine == "A":
+                nc.scalar.copy(out=out, in_=in_)
+            elif engine == "V":
+                nc.vector.tensor_copy(out=out, in_=in_)
+            else:
+                nc.gpsimd.tensor_scalar(out=out, in0=in_, scalar1=1.0, scalar2=0.0, op0=ALU.mult, op1=ALU.add)
+
+        def x1(u, a, engine):
             if a == 0:
                 tin[u] = work.tile([P, 512, 4], BF16, name="tin", align_bytes=64)
-            nc.gpsimd.tensor_scalar(
-                out=tin[u][:, a * P : (a + 1) * P, :],
-                in0=dq[u][:, :, a * P : (a + 1) * P].rearrange("p j f -> p f j"),
-                scalar1=1.0,
-                scalar2=0.0,
-                op0=ALU.mult,
-                op1=ALU.add,
+            cols = slice(a * P, (a + 1) * P)
+            interleave(tin[u][:, cols, :], dq[u][:, :, cols].rearrange("p j f -> p f j"), engine)
+
+        def quant_f(u, half):
+            G, h = ORD[u]
+            cols = slice(512 * h + 256 * half, 512 * h + 256 * half + 256)
+            nc.vector.quantize_mx(
+                out=f_codes[G][:, cols].bitcast(E5M2), scales=f_scales[G][:, cols], in_=xin[u][:, half * 1024 : half * 1024 + 1024]
             )
 
-        def quant_f(u):
-            G, h = divmod(u, 2)
-            cols = slice(512 * h, 512 * h + 512)
-            nc.vector.quantize_mx(out=f_codes[G][:, cols].bitcast(E5M2), scales=f_scales[G][:, cols], in_=xin[u][:])
-
-        def quant_t(u):
-            tcod = work.tile([P, 512], U32, name="tcod", bufs=4, align_bytes=64)
-            tsca = work.tile([P, 512], U8, name="tsca", bufs=4, align_bytes=64)
-            nc.vector.quantize_mx(out=tcod[:].bitcast(E5M2), scales=tsca[:], in_=tin[u][:].rearrange("p f j -> p (f j)"))
-            t_codes[u] = tcod
-            t_scales[u] = tsca
+        def quant_t(u, a0, a1):
+            if a0 == 0:
+                t_codes[u] = work.tile([P, 512], U32, name="tcod", bufs=CFG["tb"], align_bytes=64)
+                t_scales[u] = work.tile([P, 512], U8, name="tsca", bufs=CFG["tb"], align_bytes=64)
+            cols = slice(a0 * P, a1 * P)
+            nc.vector.quantize_mx(
+                out=t_codes[u][:, cols].bitcast(E5M2), scales=t_scales[u][:, cols], in_=tin[u][:, cols, :].rearrange("p f j -> p (f j)")
+            )
 
         mixed = {}
+        MN = CFG["mixn"]
 
-        def mix(key, n):
-            t = work.tile([P, 512, 4], BF16, name="mixed", align_bytes=64)
-            nc.scalar.copy(out=t[:], in_=raw_tiles[key][:, :, n * 512 : (n + 1) * 512].rearrange("p j c -> p c j"))
+        def mix(key, n, engine):
+            t = work.tile([P, MN, 4], BF16, name="mixed", align_bytes=64, bufs=CFG["mixb"])
+            interleave(t[:], raw_tiles[key][:, :, n * MN : (n + 1) * MN].rearrange("p j c -> p c j"), engine)
             mixed[key, n] = t
 
         def quant_w(key, n):
             kind, i = key
             codes = (x_codes if kind == "x" else w_codes)[i]
             scales = (x_scales if kind == "x" else w_scales)[i]
-            cols = slice(n * 512, (n + 1) * 512)
+            cols = slice(n * MN, (n + 1) * MN)
             nc.vector.quantize_mx(
                 out=codes[:, cols].bitcast(E4M3), scales=scales[:, cols], in_=mixed[key, n][:].rearrange("p c j -> p (c j)")
             )
@@ -259,7 +285,7 @@ def tile_mla_pb_v_kernel(tc, x, wq, q_norm_w, freqs_cos, freqs_sin, q, rstd, gra
         stage = {}
 
         def mx_group(lhs, rhs, n, key, store, engine):
-            acc = psum.tile([P, 512], F32, name="acc", tag="mx", bufs=2)
+            acc = psum.tile([P, 512], F32, name="acc", tag="mx", bufs=CFG["mxb"])
             k = len(lhs)
             for i in range(k):
                 (lc, ls, l0), (rc, rs) = lhs[i], rhs[i]
@@ -283,7 +309,7 @@ def tile_mla_pb_v_kernel(tc, x, wq, q_norm_w, freqs_cos, freqs_sin, q, rstd, gra
                 nc.sync.dma_start(out=store, in_=stage[key][:])
 
         def dw_group(G, a, n, engine=0):
-            lhs = [(t_codes[2 * G + h], t_scales[2 * G + h], a * P) for h in range(2)]
+            lhs = [(t_codes[ORD.index((G, h))], t_scales[ORD.index((G, h))], a * P) for h in range(2)]
             rhs = [(x_codes[h], x_scales[h]) for h in range(2)]
             r0 = (4 * G + a) * P
             mx_group(lhs, rhs, n, ("w", G, a), out_1[r0 : r0 + P, :], engine)
@@ -294,13 +320,21 @@ def tile_mla_pb_v_kernel(tc, x, wq, q_norm_w, freqs_cos, freqs_sin, q, rstd, gra
             rows = of[512 * h : 512 * h + 512, :].rearrange("(p j) c -> p j c", j=4)
             mx_group(lhs, rhs, n, ("x", h, jj), rows[:, jj, :], engine)
 
-        load_at = {0: [("x", 0)], 1: [("x", 1)], 2: [2], 5: [("w", 0)], 6: [3], 7: [("w", 1)], 9: [("w", 2)], 10: [4], 11: [("w", 3)], 14: [5], 18: [6], 22: [7]}
+        load_at = {}
+        for item in CFG["ls"].split():
+            i, item = item.split(":")
+            load_at.setdefault(int(i), []).append(int(item) if len(item) == 1 else (item[0], int(item[1])))
+        keys = [(v[0], int(v[1])) for v in CFG["kx"]]
+        mix_list = [(key, n) for key in keys for n in range(C // MN)]
         mix_at = {}
-        for i, (key, n) in enumerate([(("x", h), n) for h in range(2) for n in range(2)] + [(("w", G), n) for G in range(NG) for n in range(2)]):
-            mix_at[3 + i] = (key, n)
+        msteps = [int(v) for v in CFG["mx"].split()]
+        for k, item in enumerate(mix_list):
+            mix_at.setdefault(msteps[k * MN // 512], []).append(item + (CFG["me"][k * MN // 512],))
         mx_queue = []
+        df = CFG["fin"]
+        stages = dict(t1=(0, t1), ab=(CFG["ab"], mul_ab), gc=(CFG["gc"], gcopy), bp=(CFG["bp"], mul_b), t2=(CFG["t2"], t2), d=(CFG["d"], mul_d), red=(CFG["red"], red), kq=(CFG["kq"], mul_kq), fin=(CFG["fin"], fin))
         step = 0
-        while step < NS + 12 or mx_queue:
+        while step < NS + df + 6 or mx_queue:
             i = step
             for item in load_at.get(i, []):
                 if isinstance(item, int):
@@ -308,43 +342,50 @@ def tile_mla_pb_v_kernel(tc, x, wq, q_norm_w, freqs_cos, freqs_sin, q, rstd, gra
                 else:
                     src = xf if item[0] == "x" else wq
                     load_raw(item, src[512 * item[1] : 512 * item[1] + 512, :])
-            if 0 <= i - 2 < NS:
-                t2(i - 2)
-            if i < NS:
-                t1(i)
-            if 0 <= i - 3 < NS:
-                mul_d(i - 3)
-                red(i - 3)
-                mul_kq(i - 3)
-            if 0 <= i - 1 < NS:
-                mul_ab(i - 1)
-            if 0 <= i - 4 < NS:
-                fin(i - 4)
+            for name in CFG["order"].split():
+                off, fn = stages[name]
+                if 0 <= i - off < NS:
+                    fn(i - off)
+            if i == 1:
+                cube()
+            if i == CFG["tb1"]:
+                tables(1)
             for u in range(8):
-                if i == 4 * u + 6:
-                    t3(u, 0)
-                if i == 4 * u + 8:
-                    t3(u, 1)
-                    x1(u, 0)
-                    x1(u, 1)
-                if i == 4 * u + 9:
-                    x1(u, 2)
-                    x1(u, 3)
-                    quant_f(u)
-                if i == 4 * u + 10:
-                    quant_t(u)
-                    if u % 2 == 1:
-                        mx_queue += [("w", u // 2, a, n) for a in range(4) for n in range(2)]
-                    if u >= 6:
-                        mx_queue += [("x", u - 6, jj, n) for jj in range(4) for n in range(2)]
-            if i in mix_at:
-                mix(*mix_at[i])
-            if i - 1 in mix_at:
-                quant_w(*mix_at[i - 1])
-            tail = i > NS + 4
-            for b in range(4 if tail else 2):
-                if mx_queue:
+                last = u == 7
+                base = 4 * u + df
+                for half in range(2):
+                    if i == base + 2 * half + 1 + CFG["t3a"]:
+                        t3(u, half)
+                    if i == base + 2 * half + 1 + CFG["t3a"] + CFG["qf"]:
+                        quant_f(u, half)
+                        h = ORD[u][1]
+                        if all(ORD.index((G, h)) <= u for G in range(NG)):
+                            mx_queue += [("x", h, 2 * half + b, n) for b in range(2) for n in range(2)]
+                if not last:
+                    per = CFG["x1per"]
+                    for a in range(4):
+                        if i == base + 4 + a // per:
+                            x1(u, a, "G")
+                    if i == base + 4 + 4 // per:
+                        quant_t(u, 0, 4)
+                        G = ORD[u][0]
+                        if all(ORD.index((G, h)) <= u for h in range(2)):
+                            mx_queue += [("w", G, a, n) for a in range(4) for n in range(2)]
+                elif i == base + 4:
+                    for a in range(4):
+                        x1(u, a, "VAGV"[a])
+                    for a in range(4):
+                        quant_t(u, a, a + 1)
+                    mx_queue = [("w", ORD[u][0], a, n) for a in range(4) for n in range(2)] + mx_queue
+            for item in mix_at.get(i, []):
+                mix(*item)
+            for item in mix_at.get(i - CFG["qw"], []):
+                quant_w(*item[:2])
+            tail = i > NS + df - 1
+            left = 4 * CFG["tw"] if tail else CFG["bud"]
+            while mx_queue and left > 0:
                     kind, i0, i1, n = mx_queue.pop(0)
+                    left -= 2 if kind == "w" else 4
                     engine = n if tail else 0
                     if kind == "w":
                         dw_group(i0, i1, n, engine)

@@ -17,7 +17,7 @@ FLOPS = 2 * 2 * T * C * H * D
 P = 128
 NG = 4
 NS = 32
-CFG = {'ord': [(0, 0), (0, 1), (1, 0), (1, 1), (2, 0), (3, 0), (2, 1), (3, 1)], 'bud': 4, 'kx': ['x0', 'x1', 'w0', 'w1', 'w2', 'w3'], 'tb1': 3, 'hb': 0, 'gsb': 2, 'abb': 3, 'gc': 0, 'bp': 1, 'ab': 1, 't2': 2, 'd': 3, 'red': 3, 'kq': 3, 'fin': 4, 'order': 't1 gc bp t2 d red ab kq fin', 'kqe': 'A', 'mixe': 'G', 'gTb': 1, 'dhb': 3, 'xtb': 1, 'mxb': 3, 'mix0': 2, 'mixn': 512, 'qw': 2, 'perstep': 2, 'xl': 1, 'gbuf': 3, 'kqb': 4, 'mixwait': 1, 'x1per': 1, 't3a': 1, 'qf': 2, 'tb': 6, 'ls': '0:x0 1:x1 2:2 5:w0 6:3 8:w1 10:4 11:w2 14:5 15:w3 18:6 22:7', 'mx': '2 4 6 8 10 12 14 16 18 20 22 24', 'me': 'GAGAGAGAGAGA', 'tw': 2, 'mixb': 2}
+CFG = {'tt': 1, 'pb': 3, 'dm': 'D', 'xe': 'GGGG', 'part': 0, 'ob': 4, 'lt': 1, 'lq': 1, 'ebud': 6, 'ord': [(0, 0), (0, 1), (1, 0), (1, 1), (2, 0), (3, 0), (2, 1), (3, 1)], 'bud': 3, 'kx': ['x0', 'x1', 'w0', 'w1', 'w2', 'w3'], 'tb1': 1, 'hb': 0, 'gsb': 2, 'abb': 3, 'gc': 0, 'bp': 1, 'ab': 2, 't2': 4, 'd': 5, 'red': 5, 'kq': 5, 'fin': 6, 'order': 'ab t2 d t1 red bp kq gc fin', 'kqe': 'A', 'mixe': 'G', 'gTb': 2, 'dhb': 3, 'xtb': 1, 'mxb': 2, 'mix0': 2, 'mixn': 256, 'qw': 2, 'perstep': 2, 'xl': 1, 'gbuf': 3, 'kqb': 3, 'mixwait': 1, 'x1per': 2, 't3a': 0, 'qf': 1, 'tb': 6, 'ls': '0:x0 1:x1 3:2 5:w0 8:3 8:w1 11:w2 12:4 15:w3 16:5 20:6 24:7', 'mx': '3 4 6 8 10 12 14 16 18 20 22 24', 'me': 'AAGAAGAAGAAG', 'tw': 1, 'mixb': 3}
 
 
 def tile_mla_pb_v_kernel(tc, x, wq, q_norm_w, freqs_cos, freqs_sin, q, rstd, grad_out, out_0, out_1):
@@ -81,26 +81,25 @@ def tile_mla_pb_v_kernel(tc, x, wq, q_norm_w, freqs_cos, freqs_sin, q, rstd, gra
 
         wsrow = const.tile([P, 64, 2], BF16, name="wsrow")
         wv = wrow[:].rearrange("p (a e) -> p a e", e=2)
-        nc.vector.tensor_scalar(out=wsrow[:, :, 0], in0=wv[:, :, 1], scalar1=-1.0, scalar2=None, op0=ALU.mult)
-        nc.vector.tensor_copy(out=wsrow[:, :, 1], in_=wv[:, :, 0])
+        nc.scalar.activation(out=wsrow[:, :, 0], in_=wv[:, :, 1], func=ACTF.Copy, scale=-1.0)
+        nc.scalar.copy(out=wsrow[:, :, 1], in_=wv[:, :, 0])
 
         tab = const.tile([P, 2, 2, 4, P], F32, name="tab")
 
-        def tables(h):
-            for k in range(2):
-                src = (cosr, sinr)[k]
-                gain = (wv, wsrow[:])[k]
-                tok = work.tile([P, 4, 64, 2], F32, name="tok")
-                nc.vector.tensor_tensor(
-                    out=tok[:],
-                    in0=src[:, h, :, :].unsqueeze(3).to_broadcast([P, 4, 64, 2]),
-                    in1=gain.unsqueeze(1).to_broadcast([P, 4, 64, 2]),
-                    op=ALU.mult,
-                )
-                pt = psum.tile([P, 4, P], F32, name="pt", tag="dh", bufs=CFG["dhb"])
-                for jj in range(4):
-                    nc.tensor.transpose(pt[:, jj, :], tok[:, jj, :, :].rearrange("p a e -> p (a e)"), ident[:])
-                nc.scalar.copy(out=tab[:, k, h, :, :], in_=pt[:])
+        def table(h, k, engine):
+            src = (cosr, sinr)[k]
+            gain = (wv, wsrow[:])[k]
+            tok = work.tile([P, 4, 64, 2], F32, name="tok")
+            engine.tensor_tensor(
+                out=tok[:],
+                in0=src[:, h, :, :].unsqueeze(3).to_broadcast([P, 4, 64, 2]),
+                in1=gain.unsqueeze(1).to_broadcast([P, 4, 64, 2]),
+                op=ALU.mult,
+            )
+            pt = psum.tile([P, 4, P], F32, name="pt", tag="dh", bufs=CFG["dhb"])
+            for jj in range(4):
+                nc.tensor.transpose(pt[:, jj, :], tok[:, jj, :, :].rearrange("p a e -> p (a e)"), ident[:])
+            nc.scalar.copy(out=tab[:, k, h, :, :], in_=pt[:])
 
         r3 = const.tile([P, 2 * 4 * H], F32, name="r3")
         r2 = const.tile([P, 2 * 4 * H], F32, name="r2")
@@ -110,7 +109,6 @@ def tile_mla_pb_v_kernel(tc, x, wq, q_norm_w, freqs_cos, freqs_sin, q, rstd, gra
             nc.vector.tensor_tensor(out=r2[:], in0=rflat, in1=rflat, op=ALU.mult)
             nc.vector.scalar_tensor_tensor(out=r3[:], in0=r2[:], scalar=-1.0 / D, in1=rflat, op0=ALU.mult, op1=ALU.mult)
 
-        tables(0)
 
         x_codes = [const.tile([P, C], U32, name="xc%d" % h, align_bytes=64) for h in range(2)]
         x_scales = [const.tile([P, C], U8, name="xs%d" % h, align_bytes=64) for h in range(2)]
@@ -183,12 +181,29 @@ def tile_mla_pb_v_kernel(tc, x, wq, q_norm_w, freqs_cos, freqs_sin, q, rstd, gra
 
         def mul_d(s):
             u, jj, G, h = where(s)
-            t = work.tile([P, 4, P], F32, name="prod", bufs=3)
-            nc.vector.tensor_tensor(out=t[:], in0=dh[s][:], in1=q_tiles[u][:, jj, :].rearrange("p (a d) -> p a d", a=4), op=ALU.mult)
+            qv = q_tiles[u][:, jj, :].rearrange("p (a d) -> p a d", a=4)
+            t = work.tile([P, 4, P], F32, name="prod", bufs=CFG["pb"])
+            if CFG["dm"] != "F":
+                nc.vector.tensor_tensor(out=t[:], in0=dh[s][:], in1=qv, op=ALU.mult)
             prod[s] = t
+            if CFG["dm"] == "F":
+                kcol[s] = work.tile([P, 4], F32, name="kcol", bufs=4)
+                for a in range(4):
+                    col = (h * 4 + jj) * H + 4 * G + a
+                    nc.vector.scalar_tensor_tensor(
+                        out=t[:, a, :],
+                        in0=dh[s][:, a, :],
+                        scalar=r3[:, col : col + 1],
+                        in1=qv[:, a, :],
+                        op0=ALU.mult,
+                        op1=ALU.mult,
+                        accum_out=kcol[s][:, a : a + 1],
+                    )
 
         def red(s):
             u, jj, G, h = where(s)
+            if CFG["dm"] == "F":
+                return
             t = work.tile([P, 4], F32, name="kcol", bufs=4)
             junk = work.tile([P, 4, P], BF16, name="junk", bufs=3)
             for a in range(4):
@@ -201,7 +216,14 @@ def tile_mla_pb_v_kernel(tc, x, wq, q_norm_w, freqs_cos, freqs_sin, q, rstd, gra
         def mul_kq(s):
             u, jj, G, h = where(s)
             t = work.tile([P, 4, P], F32, name="kq", bufs=CFG["kqb"])
-            for a in range(4):
+            if CFG["kqe"] == "T":
+                nc.gpsimd.tensor_tensor(
+                    out=t[:],
+                    in0=q_tiles[u][:, jj, :].rearrange("p (a d) -> p a d", a=4),
+                    in1=kcol[s][:].unsqueeze(2).to_broadcast([P, 4, P]),
+                    op=ALU.mult,
+                )
+            for a in range(4 if CFG["kqe"] != "T" else 0):
                 src = q_tiles[u][:, jj, a * P : (a + 1) * P]
                 if CFG["kqe"] == "A":
                     nc.scalar.activation(out=t[:, a, :], in_=src, func=ACTF.Copy, scale=kcol[s][:, a : a + 1])
@@ -236,10 +258,13 @@ def tile_mla_pb_v_kernel(tc, x, wq, q_norm_w, freqs_cos, freqs_sin, q, rstd, gra
             nc.scalar.copy(out=dst.rearrange("p (a r v) -> p a r v", a=2, v=2), in_=pt[:].rearrange("p a v r -> p a r v"))
 
         def interleave(out, in_, engine):
-            if engine == "A":
-                nc.scalar.copy(out=out, in_=in_)
-            elif engine == "V":
-                nc.vector.tensor_copy(out=out, in_=in_)
+            if engine in "AV":
+                dst = out.rearrange("p (c i) j -> p c j i", i=4)
+                src = in_.rearrange("p (c i) j -> p c j i", i=4)
+                if engine == "A":
+                    nc.scalar.copy(out=dst, in_=src)
+                else:
+                    nc.vector.tensor_copy(out=dst, in_=src)
             else:
                 nc.gpsimd.tensor_scalar(out=out, in0=in_, scalar1=1.0, scalar2=0.0, op0=ALU.mult, op1=ALU.add)
 
@@ -270,6 +295,19 @@ def tile_mla_pb_v_kernel(tc, x, wq, q_norm_w, freqs_cos, freqs_sin, q, rstd, gra
 
         def mix(key, n, engine):
             t = work.tile([P, MN, 4], BF16, name="mixed", align_bytes=64, bufs=CFG["mixb"])
+            if engine in "PQ":
+                for c in range(MN // 256):
+                    pt = psum.tile([P, 256, 4], BF16, name="pi", tag="mx", bufs=CFG["mxb"])
+                    for j in range(4):
+                        c0 = n * MN + c * 256
+                        nc.tensor.matmul(pt[:, :, j], lhsT=identb[:], rhs=raw_tiles[key][:, j, c0 : c0 + 256], start=True, stop=True)
+                    dst = t[:, c * 256 : (c + 1) * 256, :]
+                    if engine == "P":
+                        nc.scalar.copy(out=dst, in_=pt[:])
+                    else:
+                        nc.vector.tensor_copy(out=dst, in_=pt[:])
+                mixed[key, n] = t
+                return
             interleave(t[:], raw_tiles[key][:, :, n * MN : (n + 1) * MN].rearrange("p j c -> p c j"), engine)
             mixed[key, n] = t
 
@@ -284,8 +322,12 @@ def tile_mla_pb_v_kernel(tc, x, wq, q_norm_w, freqs_cos, freqs_sin, q, rstd, gra
 
         stage = {}
 
-        def mx_group(lhs, rhs, n, key, store, engine):
-            acc = psum.tile([P, 512], F32, name="acc", tag="mx", bufs=CFG["mxb"])
+        tags = [("mx", CFG["mxb"])]
+
+        def mx_group(lhs, rhs, n, key, store, engine, add=None):
+            tag, bufs = tags[0]
+            tags.append(tags.pop(0))
+            acc = psum.tile([P, 512], F32, name="acc", tag=tag, bufs=bufs)
             k = len(lhs)
             for i in range(k):
                 (lc, ls, l0), (rc, rs) = lhs[i], rhs[i]
@@ -298,10 +340,15 @@ def tile_mla_pb_v_kernel(tc, x, wq, q_norm_w, freqs_cos, freqs_sin, q, rstd, gra
                     start=(i == 0),
                     stop=(i == k - 1),
                 )
+            if store is None:
+                nc.scalar.copy(out=add, in_=acc[:])
+                return
             if n == 0:
-                stage[key] = work.tile([P, C], F32, name="ostage", bufs=3)
+                stage[key] = work.tile([P, C], F32, name="ostage", bufs=CFG["ob"])
             dst = stage[key][:, n * 512 : (n + 1) * 512]
-            if engine == 0:
+            if add is not None:
+                nc.vector.tensor_tensor(out=dst, in0=acc[:], in1=add, op=ALU.add)
+            elif engine == 0:
                 nc.scalar.copy(out=dst, in_=acc[:])
             else:
                 nc.vector.tensor_copy(out=dst, in_=acc[:])
@@ -314,12 +361,16 @@ def tile_mla_pb_v_kernel(tc, x, wq, q_norm_w, freqs_cos, freqs_sin, q, rstd, gra
             r0 = (4 * G + a) * P
             mx_group(lhs, rhs, n, ("w", G, a), out_1[r0 : r0 + P, :], engine)
 
-        def dx_group(h, jj, n, engine=0):
-            lhs = [(f_codes[G], f_scales[G], h * 512 + jj * P) for G in range(NG)]
-            rhs = [(w_codes[G], w_scales[G]) for G in range(NG)]
+        def dx_group(h, jj, n, engine=0, Gs=range(NG), add=None, store=True):
+            lhs = [(f_codes[G], f_scales[G], h * 512 + jj * P) for G in Gs]
+            rhs = [(w_codes[G], w_scales[G]) for G in Gs]
             rows = of[512 * h : 512 * h + 512, :].rearrange("(p j) c -> p j c", j=4)
-            mx_group(lhs, rhs, n, ("x", h, jj), rows[:, jj, :], engine)
+            mx_group(lhs, rhs, n, ("x", h, jj), rows[:, jj, :] if store else None, engine, add)
 
+        part = const.tile([P, 4, C], F32, name="part") if CFG["part"] else None
+        HL = ORD[7][1]
+        GL = ORD[7][0]
+        GP = [G for G in range(NG) if G != GL]
         load_at = {}
         for item in CFG["ls"].split():
             i, item = item.split(":")
@@ -333,6 +384,9 @@ def tile_mla_pb_v_kernel(tc, x, wq, q_norm_w, freqs_cos, freqs_sin, q, rstd, gra
         mx_queue = []
         df = CFG["fin"]
         stages = dict(t1=(0, t1), ab=(CFG["ab"], mul_ab), gc=(CFG["gc"], gcopy), bp=(CFG["bp"], mul_b), t2=(CFG["t2"], t2), d=(CFG["d"], mul_d), red=(CFG["red"], red), kq=(CFG["kq"], mul_kq), fin=(CFG["fin"], fin))
+        table(ORD[0][1], 0, nc.vector)
+        t1(0)
+        table(ORD[0][1], 1, nc.vector)
         step = 0
         while step < NS + df + 6 or mx_queue:
             i = step
@@ -344,28 +398,33 @@ def tile_mla_pb_v_kernel(tc, x, wq, q_norm_w, freqs_cos, freqs_sin, q, rstd, gra
                     load_raw(item, src[512 * item[1] : 512 * item[1] + 512, :])
             for name in CFG["order"].split():
                 off, fn = stages[name]
-                if 0 <= i - off < NS:
+                if 0 <= i - off < NS and (name != "t1" or i > 0):
                     fn(i - off)
             if i == 1:
                 cube()
             if i == CFG["tb1"]:
-                tables(1)
+                table(1 - ORD[0][1], 0, nc.gpsimd)
+                table(1 - ORD[0][1], 1, nc.gpsimd)
             for u in range(8):
                 last = u == 7
                 base = 4 * u + df
                 for half in range(2):
-                    if i == base + 2 * half + 1 + CFG["t3a"]:
+                    ia = base + 2 * half + 1 + (CFG["lt"] if last else CFG["t3a"])
+                    if i == ia:
                         t3(u, half)
-                    if i == base + 2 * half + 1 + CFG["t3a"] + CFG["qf"]:
+                    if i == ia + (CFG["lq"] if last else CFG["qf"]):
                         quant_f(u, half)
                         h = ORD[u][1]
                         if all(ORD.index((G, h)) <= u for G in range(NG)):
-                            mx_queue += [("x", h, 2 * half + b, n) for b in range(2) for n in range(2)]
+                            kind = "f" if CFG["part"] and h == HL else "x"
+                            mx_queue += [(kind, h, 2 * half + b, n) for b in range(2) for n in range(2)]
+                        elif CFG["part"] and h == HL and all(ORD.index((G, h)) <= u for G in GP):
+                            mx_queue += [("p", h, 2 * half + b, n) for b in range(2) for n in range(2)]
                 if not last:
                     per = CFG["x1per"]
                     for a in range(4):
                         if i == base + 4 + a // per:
-                            x1(u, a, "G")
+                            x1(u, a, CFG["xe"][a])
                     if i == base + 4 + 4 // per:
                         quant_t(u, 0, 4)
                         G = ORD[u][0]
@@ -382,13 +441,19 @@ def tile_mla_pb_v_kernel(tc, x, wq, q_norm_w, freqs_cos, freqs_sin, q, rstd, gra
             for item in mix_at.get(i - CFG["qw"], []):
                 quant_w(*item[:2])
             tail = i > NS + df - 1
-            left = 4 * CFG["tw"] if tail else CFG["bud"]
+            if i == NS + df and CFG["tt"]:
+                DH, GT, MX = ("dh", CFG["dhb"]), ("gT", CFG["gTb"]), ("mx", CFG["mxb"])
+                tags[:] = [DH, GT, MX, DH, GT, MX, DH]
+            left = 4 * CFG["tw"] if tail else (CFG["ebud"] if i >= NS else CFG["bud"])
             while mx_queue and left > 0:
                     kind, i0, i1, n = mx_queue.pop(0)
-                    left -= 2 if kind == "w" else 4
+                    left -= {"w": 2, "x": 4, "p": 3, "f": 1}[kind]
                     engine = n if tail else 0
                     if kind == "w":
                         dw_group(i0, i1, n, engine)
-                    else:
+                    elif kind == "x":
                         dx_group(i0, i1, n, engine)
+                    else:
+                        pc = part[:, i1, n * 512 : (n + 1) * 512]
+                        dx_group(i0, i1, n, engine, GP if kind == "p" else [GL], pc, kind == "f")
             step += 1

@@ -17,7 +17,7 @@ FLOPS = 2 * 2 * T * C * H * D
 P = 128
 NG = 4
 NS = 32
-CFG = {'tt': 1, 'pb': 3, 'dm': 'D', 'xe': 'GGGG', 'part': 0, 'ob': 4, 'lt': 1, 'lq': 1, 'ebud': 6, 'ord': [(0, 0), (0, 1), (1, 0), (1, 1), (2, 0), (3, 0), (2, 1), (3, 1)], 'bud': 3, 'kx': ['x0', 'x1', 'w0', 'w1', 'w2', 'w3'], 'tb1': 1, 'hb': 0, 'gsb': 2, 'abb': 3, 'gc': 0, 'bp': 1, 'ab': 2, 't2': 4, 'd': 5, 'red': 5, 'kq': 5, 'fin': 6, 'order': 'ab t2 d t1 red bp kq gc fin', 'kqe': 'A', 'mixe': 'G', 'gTb': 2, 'dhb': 3, 'xtb': 1, 'mxb': 2, 'mix0': 2, 'mixn': 256, 'qw': 2, 'perstep': 2, 'xl': 1, 'gbuf': 3, 'kqb': 3, 'mixwait': 1, 'x1per': 2, 't3a': 0, 'qf': 1, 'tb': 6, 'ls': '0:x0 1:x1 3:2 5:w0 8:3 8:w1 11:w2 12:4 15:w3 16:5 20:6 24:7', 'mx': '3 4 6 8 10 12 14 16 18 20 22 24', 'me': 'AAGAAGAAGAAG', 'tw': 1, 'mixb': 3}
+CFG = {'ts': 1, 'cu': 2, 'abm': 1, 'qfm': 1, 'qwm': 1, 'tkb': 4, 'kqh': 0, 'tt': 1, 'pb': 3, 'dm': 'D', 'xe': 'GGGG', 'part': 0, 'ob': 4, 'lt': 1, 'lq': 1, 'ebud': 6, 'ord': [(0, 0), (0, 1), (1, 0), (1, 1), (2, 0), (3, 0), (2, 1), (3, 1)], 'bud': 3, 'kx': ['x0', 'x1', 'w0', 'w1', 'w2', 'w3'], 'tb1': 1, 'hb': 1, 'gsb': 3, 'abb': 4, 'gc': 1, 'bp': 1, 'ab': 2, 't2': 4, 'd': 5, 'red': 5, 'kq': 5, 'fin': 6, 'order': 'gc bp ab t2 d t1 red kq fin', 'kqe': 'A', 'mixe': 'G', 'gTb': 2, 'dhb': 3, 'xtb': 1, 'mxb': 2, 'mix0': 2, 'mixn': 512, 'qw': 2, 'perstep': 2, 'xl': 1, 'gbuf': 3, 'kqb': 3, 'mixwait': 1, 'x1per': 2, 't3a': 0, 'qf': 1, 'tb': 6, 'ls': '0:x0 1:x1 3:2 5:w0 8:3 8:w1 11:w2 12:4 15:w3 16:5 20:6 24:7', 'mx': '3 4 6 8 10 12 14 16 18 20 22 24', 'me': 'GAGAGAGAGAGA', 'tw': 1, 'mixb': 3}
 
 
 def tile_mla_pb_v_kernel(tc, x, wq, q_norm_w, freqs_cos, freqs_sin, q, rstd, grad_out, out_0, out_1):
@@ -34,7 +34,6 @@ def tile_mla_pb_v_kernel(tc, x, wq, q_norm_w, freqs_cos, freqs_sin, q, rstd, gra
         loads = ctx.enter_context(tc.tile_pool(name="loads", bufs=3))
         work = ctx.enter_context(tc.tile_pool(name="work", bufs=2))
         psum = ctx.enter_context(tc.psum_pool(name="psum", bufs=1))
-        ctx.enter_context(tc.manual_schedule())
 
         wrow = const.tile([P, D], BF16, name="wrow")
         nc.sync.dma_start(out=wrow[:], in_=q_norm_w.partition_broadcast(P))
@@ -86,20 +85,21 @@ def tile_mla_pb_v_kernel(tc, x, wq, q_norm_w, freqs_cos, freqs_sin, q, rstd, gra
 
         tab = const.tile([P, 2, 2, 4, P], F32, name="tab")
 
-        def table(h, k, engine):
+        def table(h, k, engine, j0=0, j1=4):
             src = (cosr, sinr)[k]
             gain = (wv, wsrow[:])[k]
-            tok = work.tile([P, 4, 64, 2], F32, name="tok")
+            n = j1 - j0
+            tok = work.tile([P, n, 64, 2], F32, name="tok", bufs=CFG["tkb"])
             engine.tensor_tensor(
                 out=tok[:],
-                in0=src[:, h, :, :].unsqueeze(3).to_broadcast([P, 4, 64, 2]),
-                in1=gain.unsqueeze(1).to_broadcast([P, 4, 64, 2]),
+                in0=src[:, h, j0:j1, :].unsqueeze(3).to_broadcast([P, n, 64, 2]),
+                in1=gain.unsqueeze(1).to_broadcast([P, n, 64, 2]),
                 op=ALU.mult,
             )
-            pt = psum.tile([P, 4, P], F32, name="pt", tag="dh", bufs=CFG["dhb"])
-            for jj in range(4):
+            pt = psum.tile([P, n, P], F32, name="pt", tag="dh", bufs=CFG["dhb"])
+            for jj in range(n):
                 nc.tensor.transpose(pt[:, jj, :], tok[:, jj, :, :].rearrange("p a e -> p (a e)"), ident[:])
-            nc.scalar.copy(out=tab[:, k, h, :, :], in_=pt[:])
+            nc.scalar.copy(out=tab[:, k, h, j0:j1, :], in_=pt[:])
 
         r3 = const.tile([P, 2 * 4 * H], F32, name="r3")
         r2 = const.tile([P, 2 * 4 * H], F32, name="r2")
@@ -163,6 +163,14 @@ def tile_mla_pb_v_kernel(tc, x, wq, q_norm_w, freqs_cos, freqs_sin, q, rstd, gra
 
         def mul_ab(s):
             u, jj, G, h = where(s)
+            if not HB and CFG["abm"]:
+                nc.vector.tensor_tensor(
+                    out=ab[s][:],
+                    in0=gT[s][:].unsqueeze(1).to_broadcast([P, 2, 4, P]),
+                    in1=tab[:, :, h, jj, :].unsqueeze(2).to_broadcast([P, 2, 4, P]),
+                    op=ALU.mult,
+                )
+                return
             for k in range(2):
                 hh = 4 - HB * k
                 nc.vector.tensor_tensor(
@@ -225,7 +233,7 @@ def tile_mla_pb_v_kernel(tc, x, wq, q_norm_w, freqs_cos, freqs_sin, q, rstd, gra
                 )
             for a in range(4 if CFG["kqe"] != "T" else 0):
                 src = q_tiles[u][:, jj, a * P : (a + 1) * P]
-                if CFG["kqe"] == "A":
+                if CFG["kqe"] == "A" and a < 4 - CFG["kqh"]:
                     nc.scalar.activation(out=t[:, a, :], in_=src, func=ACTF.Copy, scale=kcol[s][:, a : a + 1])
                 else:
                     nc.gpsimd.tensor_scalar(out=t[:, a, :], in0=src, scalar1=kcol[s][:, a : a + 1], scalar2=0.0, op0=ALU.mult, op1=ALU.add)
@@ -276,9 +284,14 @@ def tile_mla_pb_v_kernel(tc, x, wq, q_norm_w, freqs_cos, freqs_sin, q, rstd, gra
 
         def quant_f(u, half):
             G, h = ORD[u]
-            cols = slice(512 * h + 256 * half, 512 * h + 256 * half + 256)
+            w0, w1 = 256 * half, 256 * half + 256
+            if CFG["qfm"] and u < 7:
+                w0 = 0
+                if half == 0:
+                    return
+            cols = slice(512 * h + w0, 512 * h + w1)
             nc.vector.quantize_mx(
-                out=f_codes[G][:, cols].bitcast(E5M2), scales=f_scales[G][:, cols], in_=xin[u][:, half * 1024 : half * 1024 + 1024]
+                out=f_codes[G][:, cols].bitcast(E5M2), scales=f_scales[G][:, cols], in_=xin[u][:, 4 * w0 : 4 * w1]
             )
 
         def quant_t(u, a0, a1):
@@ -294,6 +307,12 @@ def tile_mla_pb_v_kernel(tc, x, wq, q_norm_w, freqs_cos, freqs_sin, q, rstd, gra
         MN = CFG["mixn"]
 
         def mix(key, n, engine):
+            if CFG["qwm"] and MN == 256:
+                if n % 2 == 0:
+                    mixed[key, n // 2] = work.tile([P, 512, 4], BF16, name="mixed", align_bytes=64, bufs=CFG["mixb"])
+                dst = mixed[key, n // 2][:, (n % 2) * 256 : (n % 2) * 256 + 256, :]
+                interleave(dst, raw_tiles[key][:, :, n * MN : (n + 1) * MN].rearrange("p j c -> p c j"), engine)
+                return
             t = work.tile([P, MN, 4], BF16, name="mixed", align_bytes=64, bufs=CFG["mixb"])
             if engine in "PQ":
                 for c in range(MN // 256):
@@ -312,10 +331,15 @@ def tile_mla_pb_v_kernel(tc, x, wq, q_norm_w, freqs_cos, freqs_sin, q, rstd, gra
             mixed[key, n] = t
 
         def quant_w(key, n):
+            QN = MN
+            if CFG["qwm"] and MN == 256:
+                if n % 2 == 0:
+                    return
+                n, QN = n // 2, 512
             kind, i = key
             codes = (x_codes if kind == "x" else w_codes)[i]
             scales = (x_scales if kind == "x" else w_scales)[i]
-            cols = slice(n * MN, (n + 1) * MN)
+            cols = slice(n * QN, (n + 1) * QN)
             nc.vector.quantize_mx(
                 out=codes[:, cols].bitcast(E4M3), scales=scales[:, cols], in_=mixed[key, n][:].rearrange("p c j -> p (c j)")
             )
@@ -384,9 +408,18 @@ def tile_mla_pb_v_kernel(tc, x, wq, q_norm_w, freqs_cos, freqs_sin, q, rstd, gra
         mx_queue = []
         df = CFG["fin"]
         stages = dict(t1=(0, t1), ab=(CFG["ab"], mul_ab), gc=(CFG["gc"], gcopy), bp=(CFG["bp"], mul_b), t2=(CFG["t2"], t2), d=(CFG["d"], mul_d), red=(CFG["red"], red), kq=(CFG["kq"], mul_kq), fin=(CFG["fin"], fin))
-        table(ORD[0][1], 0, nc.vector)
-        t1(0)
-        table(ORD[0][1], 1, nc.vector)
+        if CFG["ts"]:
+            table(ORD[0][1], 0, nc.vector, 0, 1)
+            table(ORD[0][1], 1, nc.vector, 0, 1)
+            t1(0)
+            table(ORD[0][1], 0, nc.vector, 1, 4)
+            table(ORD[0][1], 1, nc.vector, 1, 4)
+        else:
+            table(ORD[0][1], 0, nc.vector)
+            t1(0)
+            table(ORD[0][1], 1, nc.vector)
+        if CFG["cu"] < 0:
+            cube()
         step = 0
         while step < NS + df + 6 or mx_queue:
             i = step
@@ -400,7 +433,7 @@ def tile_mla_pb_v_kernel(tc, x, wq, q_norm_w, freqs_cos, freqs_sin, q, rstd, gra
                 off, fn = stages[name]
                 if 0 <= i - off < NS and (name != "t1" or i > 0):
                     fn(i - off)
-            if i == 1:
+            if i == CFG["cu"]:
                 cube()
             if i == CFG["tb1"]:
                 table(1 - ORD[0][1], 0, nc.gpsimd)
@@ -415,11 +448,13 @@ def tile_mla_pb_v_kernel(tc, x, wq, q_norm_w, freqs_cos, freqs_sin, q, rstd, gra
                     if i == ia + (CFG["lq"] if last else CFG["qf"]):
                         quant_f(u, half)
                         h = ORD[u][1]
-                        if all(ORD.index((G, h)) <= u for G in range(NG)):
+                        if CFG["qfm"] and u < 7 and half == 0:
+                            pass
+                        elif all(ORD.index((G, h)) <= u for G in range(NG)):
                             kind = "f" if CFG["part"] and h == HL else "x"
-                            mx_queue += [(kind, h, 2 * half + b, n) for b in range(2) for n in range(2)]
+                            mx_queue += [(kind, h, jj, n) for jj in range(0 if CFG["qfm"] and u < 7 else 2 * half, 2 * half + 2) for n in range(2)]
                         elif CFG["part"] and h == HL and all(ORD.index((G, h)) <= u for G in GP):
-                            mx_queue += [("p", h, 2 * half + b, n) for b in range(2) for n in range(2)]
+                            mx_queue += [("p", h, jj, n) for jj in range(0 if CFG["qfm"] and u < 7 else 2 * half, 2 * half + 2) for n in range(2)]
                 if not last:
                     per = CFG["x1per"]
                     for a in range(4):

@@ -17,7 +17,7 @@ FLOPS = 2 * 2 * T * C * H * D
 P = 128
 NG = 4
 NS = 32
-CFG = {'ts': 1, 'cu': 2, 'abm': 1, 'qfm': 1, 'qwm': 1, 'tkb': 4, 'kqh': 0, 'tt': 1, 'pb': 3, 'dm': 'D', 'xe': 'GGGG', 'part': 0, 'ob': 4, 'lt': 1, 'lq': 1, 'ebud': 6, 'ord': [(0, 0), (0, 1), (1, 0), (1, 1), (2, 0), (3, 0), (2, 1), (3, 1)], 'bud': 3, 'kx': ['x0', 'x1', 'w0', 'w1', 'w2', 'w3'], 'tb1': 1, 'hb': 1, 'gsb': 3, 'abb': 4, 'gc': 1, 'bp': 1, 'ab': 2, 't2': 4, 'd': 5, 'red': 5, 'kq': 5, 'fin': 6, 'order': 'gc bp ab t2 d t1 red kq fin', 'kqe': 'A', 'mixe': 'G', 'gTb': 2, 'dhb': 3, 'xtb': 1, 'mxb': 2, 'mix0': 2, 'mixn': 512, 'qw': 2, 'perstep': 2, 'xl': 1, 'gbuf': 3, 'kqb': 3, 'mixwait': 1, 'x1per': 2, 't3a': 0, 'qf': 1, 'tb': 6, 'ls': '0:x0 1:x1 3:2 5:w0 8:3 8:w1 11:w2 12:4 15:w3 16:5 20:6 24:7', 'mx': '3 4 6 8 10 12 14 16 18 20 22 24', 'me': 'GAGAGAGAGAGA', 'tw': 1, 'mixb': 3}
+CFG = {'ts': 1, 'cu': 2, 'abm': 0, 'qfm': 0, 'qwm': 1, 'tkb': 4, 'kqh': 0, 'tt': 1, 'pb': 3, 'dm': 'D', 'xe': 'GGGG', 'part': 0, 'ob': 4, 'lt': 1, 'lq': 1, 'ebud': 6, 'ord': [(0, 0), (0, 1), (1, 0), (1, 1), (2, 0), (3, 0), (2, 1), (3, 1)], 'bud': 3, 'kx': ['x0', 'x1', 'w0', 'w1', 'w2', 'w3'], 'tb1': 1, 'hb': 0, 'gsb': 2, 'abb': 3, 'gc': 0, 'bp': 1, 'ab': 2, 't2': 4, 'd': 5, 'red': 5, 'kq': 5, 'fin': 6, 'order': 'ab t2 d t1 red bp kq gc fin', 'kqe': 'A', 'mixe': 'G', 'gTb': 2, 'dhb': 3, 'xtb': 1, 'mxb': 2, 'mix0': 2, 'mixn': 512, 'qw': 2, 'perstep': 2, 'xl': 1, 'gbuf': 3, 'kqb': 3, 'mixwait': 1, 'x1per': 2, 't3a': 0, 'qf': 1, 'tb': 6, 'ls': '0:x0 1:x1 3:2 5:w0 8:3 8:w1 11:w2 12:4 15:w3 16:5 20:6 24:7', 'mx': '3 4 6 8 10 12 14 16 18 20 22 24', 'me': 'GAGAGAGAGAGA', 'tw': 1, 'mixb': 3}
 
 
 def tile_mla_pb_v_kernel(tc, x, wq, q_norm_w, freqs_cos, freqs_sin, q, rstd, grad_out, out_0, out_1):

from contextlib import ExitStack

import concourse.mybir as mybir
from concourse.masks import make_identity

F32 = mybir.dt.float32
BF16 = mybir.dt.bfloat16
U32 = mybir.dt.uint32
U8 = mybir.dt.uint8
E4M3 = mybir.dt.float8_e4m3fn_x4
E5M2 = mybir.dt.float8_e5m2_x4
ALU = mybir.AluOpType
ACTF = mybir.ActivationFunctionType

T, C, H, D = 1024, 1024, 16, 128
FLOPS = 2 * 2 * T * C * H * D
P = 128
NG = 4
NS = 32
CFG = {'ts': 1, 'cu': 2, 'abm': 0, 'qfm': 0, 'qwm': 1, 'tkb': 4, 'kqh': 0, 'tt': 1, 'pb': 3, 'dm': 'D', 'xe': 'GGGG', 'part': 0, 'ob': 4, 'lt': 1, 'lq': 1, 'ebud': 6, 'ord': [(0, 0), (0, 1), (1, 0), (1, 1), (2, 0), (3, 0), (2, 1), (3, 1)], 'bud': 3, 'kx': ['x0', 'x1', 'w0', 'w1', 'w2', 'w3'], 'tb1': 1, 'hb': 0, 'gsb': 2, 'abb': 3, 'gc': 0, 'bp': 1, 'ab': 2, 't2': 4, 'd': 5, 'red': 5, 'kq': 5, 'fin': 6, 'order': 'ab t2 d t1 red bp kq gc fin', 'kqe': 'A', 'mixe': 'G', 'gTb': 2, 'dhb': 3, 'xtb': 1, 'mxb': 2, 'mix0': 2, 'mixn': 512, 'qw': 2, 'perstep': 2, 'xl': 1, 'gbuf': 3, 'kqb': 3, 'mixwait': 1, 'x1per': 2, 't3a': 0, 'qf': 1, 'tb': 6, 'ls': '0:x0 1:x1 3:2 5:w0 8:3 8:w1 11:w2 12:4 15:w3 16:5 20:6 24:7', 'mx': '3 4 6 8 10 12 14 16 18 20 22 24', 'me': 'GAGAGAGAGAGA', 'tw': 1, 'mixb': 3}


def tile_mla_pb_v_kernel(tc, x, wq, q_norm_w, freqs_cos, freqs_sin, q, rstd, grad_out, out_0, out_1):
    nc = tc.nc
    ORD = CFG["ord"]
    qf = q.rearrange("b t n d -> (b t) (n d)")
    gf = grad_out.rearrange("b t n d -> (b t) (n d)")
    xf = x.rearrange("b t c -> (b t) c")
    rf = rstd.rearrange("b t n -> (b t) n")
    of = out_0.rearrange("b t c -> (b t) c")

    with ExitStack() as ctx:
        const = ctx.enter_context(tc.tile_pool(name="const", bufs=1))
        loads = ctx.enter_context(tc.tile_pool(name="loads", bufs=3))
        work = ctx.enter_context(tc.tile_pool(name="work", bufs=2))
        psum = ctx.enter_context(tc.psum_pool(name="psum", bufs=1))

        wrow = const.tile([P, D], BF16, name="wrow")
        nc.sync.dma_start(out=wrow[:], in_=q_norm_w.partition_broadcast(P))
        cosr = const.tile([P, 2, 4, 64], BF16, name="cosr")
        sinr = const.tile([P, 2, 4, 64], BF16, name="sinr")
        nc.sync.dma_start(out=cosr[:], in_=freqs_cos.rearrange("(h p j) d -> p h j d", h=2, j=4))
        nc.sync.dma_start(out=sinr[:], in_=freqs_sin.rearrange("(h p j) d -> p h j d", h=2, j=4))

        g_tiles = {}
        q_tiles = {}

        def load(u):
            G, h = ORD[u]
            gt = loads.tile([P, 4, 512], BF16, name="gt")
            qt = loads.tile([P, 4, 512], F32, name="qt")
            rows = slice(512 * h, 512 * h + 512)
            cols = slice(512 * G, 512 * G + 512)
            nc.sync.dma_start(out=gt[:], in_=gf[rows, cols].rearrange("(p j) w -> p j w", j=4))
            nc.sync.dma_start(out=qt[:], in_=qf[rows, cols].rearrange("(p j) w -> p j w", j=4))
            g_tiles[u] = gt
            q_tiles[u] = qt

        raw_tiles = {}

        def load_raw(key, ap):
            rt = loads.tile([P, 4, 1024], BF16, name="raw", bufs=2)
            nc.sync.dma_start(out=rt[:], in_=ap.rearrange("(p j) c -> p j c", j=4))
            raw_tiles[key] = rt

        rst = const.tile([P, 2, 4, H], F32, name="rst")
        nc.sync.dma_start(out=rst[:], in_=rf.rearrange("(h p j) n -> p h j n", h=2, j=4))
        load(0)
        load(1)

        ident = const.tile([P, P], F32, name="ident")
        make_identity(nc, ident[:])
        identb = const.tile([P, P], BF16, name="identb")
        nc.gpsimd.tensor_copy(out=identb[:], in_=ident[:])
        swap = const.tile([P, 64, 2], F32, name="swap")
        idv = ident[:].rearrange("p (a e) -> p a e", e=2)
        nc.gpsimd.tensor_copy(out=swap[:, :, 0], in_=idv[:, :, 1])
        nc.gpsimd.tensor_copy(out=swap[:, :, 1], in_=idv[:, :, 0])
        swapf = swap[:].rearrange("p a e -> p (a e)")

        wsrow = const.tile([P, 64, 2], BF16, name="wsrow")
        wv = wrow[:].rearrange("p (a e) -> p a e", e=2)
        nc.scalar.activation(out=wsrow[:, :, 0], in_=wv[:, :, 1], func=ACTF.Copy, scale=-1.0)
        nc.scalar.copy(out=wsrow[:, :, 1], in_=wv[:, :, 0])

        tab = const.tile([P, 2, 2, 4, P], F32, name="tab")

        def table(h, k, engine, j0=0, j1=4):
            src = (cosr, sinr)[k]
            gain = (wv, wsrow[:])[k]
            n = j1 - j0
            tok = work.tile([P, n, 64, 2], F32, name="tok", bufs=CFG["tkb"])
            engine.tensor_tensor(
                out=tok[:],
                in0=src[:, h, j0:j1, :].unsqueeze(3).to_broadcast([P, n, 64, 2]),
                in1=gain.unsqueeze(1).to_broadcast([P, n, 64, 2]),
                op=ALU.mult,
            )
            pt = psum.tile([P, n, P], F32, name="pt", tag="dh", bufs=CFG["dhb"])
            for jj in range(n):
                nc.tensor.transpose(pt[:, jj, :], tok[:, jj, :, :].rearrange("p a e -> p (a e)"), ident[:])
            nc.scalar.copy(out=tab[:, k, h, j0:j1, :], in_=pt[:])

        r3 = const.tile([P, 2 * 4 * H], F32, name="r3")
        r2 = const.tile([P, 2 * 4 * H], F32, name="r2")
        rflat = rst[:].rearrange("p h j n -> p (h j n)")

        def cube():
            nc.vector.tensor_tensor(out=r2[:], in0=rflat, in1=rflat, op=ALU.mult)
            nc.vector.scalar_tensor_tensor(out=r3[:], in0=r2[:], scalar=-1.0 / D, in1=rflat, op0=ALU.mult, op1=ALU.mult)


        x_codes = [const.tile([P, C], U32, name="xc%d" % h, align_bytes=64) for h in range(2)]
        x_scales = [const.tile([P, C], U8, name="xs%d" % h, align_bytes=64) for h in range(2)]
        w_codes = [const.tile([P, C], U32, name="wc%d" % G, align_bytes=64) for G in range(NG)]
        w_scales = [const.tile([P, C], U8, name="ws%d" % G, align_bytes=64) for G in range(NG)]
        f_codes = [const.tile([P, T], U32, name="fc%d" % G, align_bytes=64) for G in range(NG)]
        f_scales = [const.tile([P, T], U8, name="fs%d" % G, align_bytes=64) for G in range(NG)]
        t_codes = {}
        t_scales = {}

        gT = {}
        ab = {}
        dh = {}
        prod = {}
        kcol = {}
        kq = {}
        dq = {}
        xin = {}
        tin = {}

        def where(s):
            u, jj = divmod(s, 4)
            G, h = ORD[u]
            return u, jj, G, h

        def t1(s):
            u, jj, G, h = where(s)
            pt = psum.tile([P, 4, P], BF16, name="gT", tag="gT", bufs=CFG["gTb"])
            for a in range(4):
                nc.tensor.transpose(pt[:, a, :], g_tiles[u][:, jj, a * P : (a + 1) * P], identb[:])
            gT[s] = pt

        HB = CFG["hb"]
        gs = {}

        def gcopy(s):
            if HB:
                t = work.tile([P, HB, P], BF16, name="gs", bufs=CFG["gsb"])
                nc.scalar.copy(out=t[:], in_=gT[s][:, 4 - HB :, :])
                gs[s] = t

        def mul_b(s):
            u, jj, G, h = where(s)
            ab[s] = work.tile([P, 2, 4, P], F32, name="ab", bufs=CFG["abb"])
            if HB:
                nc.gpsimd.tensor_tensor(
                    out=ab[s][:, 1, 4 - HB :, :],
                    in0=gs[s][:],
                    in1=tab[:, 1, h, jj, :].unsqueeze(1).to_broadcast([P, HB, P]),
                    op=ALU.mult,
                )

        def mul_ab(s):
            u, jj, G, h = where(s)
            if not HB and CFG["abm"]:
                nc.vector.tensor_tensor(
                    out=ab[s][:],
                    in0=gT[s][:].unsqueeze(1).to_broadcast([P, 2, 4, P]),
                    in1=tab[:, :, h, jj, :].unsqueeze(2).to_broadcast([P, 2, 4, P]),
                    op=ALU.mult,
                )
                return
            for k in range(2):
                hh = 4 - HB * k
                nc.vector.tensor_tensor(
                    out=ab[s][:, k, 0:hh, :],
                    in0=gT[s][:, 0:hh, :],
                    in1=tab[:, k, h, jj, :].unsqueeze(1).to_broadcast([P, hh, P]),
                    op=ALU.mult,
                )

        def t2(s):
            pt = psum.tile([P, 4, P], F32, name="dh", tag="dh", bufs=CFG["dhb"])
            for a in range(4):
                nc.tensor.matmul(pt[:, a, :], lhsT=ab[s][:, 0, a, :], rhs=ident[:], is_transpose=True, start=True, stop=False)
                nc.tensor.matmul(pt[:, a, :], lhsT=ab[s][:, 1, a, :], rhs=swapf, is_transpose=True, start=False, stop=True)
            dh[s] = pt

        def mul_d(s):
            u, jj, G, h = where(s)
            qv = q_tiles[u][:, jj, :].rearrange("p (a d) -> p a d", a=4)
            t = work.tile([P, 4, P], F32, name="prod", bufs=CFG["pb"])
            if CFG["dm"] != "F":
                nc.vector.tensor_tensor(out=t[:], in0=dh[s][:], in1=qv, op=ALU.mult)
            prod[s] = t
            if CFG["dm"] == "F":
                kcol[s] = work.tile([P, 4], F32, name="kcol", bufs=4)
                for a in range(4):
                    col = (h * 4 + jj) * H + 4 * G + a
                    nc.vector.scalar_tensor_tensor(
                        out=t[:, a, :],
                        in0=dh[s][:, a, :],
                        scalar=r3[:, col : col + 1],
                        in1=qv[:, a, :],
                        op0=ALU.mult,
                        op1=ALU.mult,
                        accum_out=kcol[s][:, a : a + 1],
                    )

        def red(s):
            u, jj, G, h = where(s)
            if CFG["dm"] == "F":
                return
            t = work.tile([P, 4], F32, name="kcol", bufs=4)
            junk = work.tile([P, 4, P], BF16, name="junk", bufs=3)
            for a in range(4):
                col = (h * 4 + jj) * H + 4 * G + a
                nc.scalar.activation(
                    out=junk[:, a, :], in_=prod[s][:, a, :], func=ACTF.Copy, scale=r3[:, col : col + 1], accum_out=t[:, a : a + 1]
                )
            kcol[s] = t

        def mul_kq(s):
            u, jj, G, h = where(s)
            t = work.tile([P, 4, P], F32, name="kq", bufs=CFG["kqb"])
            if CFG["kqe"] == "T":
                nc.gpsimd.tensor_tensor(
                    out=t[:],
                    in0=q_tiles[u][:, jj, :].rearrange("p (a d) -> p a d", a=4),
                    in1=kcol[s][:].unsqueeze(2).to_broadcast([P, 4, P]),
                    op=ALU.mult,
                )
            for a in range(4 if CFG["kqe"] != "T" else 0):
                src = q_tiles[u][:, jj, a * P : (a + 1) * P]
                if CFG["kqe"] == "A" and a < 4 - CFG["kqh"]:
                    nc.scalar.activation(out=t[:, a, :], in_=src, func=ACTF.Copy, scale=kcol[s][:, a : a + 1])
                else:
                    nc.gpsimd.tensor_scalar(out=t[:, a, :], in0=src, scalar1=kcol[s][:, a : a + 1], scalar2=0.0, op0=ALU.mult, op1=ALU.add)
            kq[s] = t

        def fin(s):
            u, jj, G, h = where(s)
            if jj == 0:
                dq[u] = work.tile([P, 4, 512], BF16, name="dq", bufs=3, align_bytes=64)
            for a in range(4):
                nc.vector.scalar_tensor_tensor(
                    out=dq[u][:, jj, a * P : (a + 1) * P],
                    in0=dh[s][:, a, :],
                    scalar=rst[:, h, jj, 4 * G + a : 4 * G + a + 1],
                    in1=kq[s][:, a, :],
                    op0=ALU.mult,
                    op1=ALU.add,
                )

        def t3(u, half):
            if half == 0:
                xin[u] = work.tile([P, 4 * P * 4], BF16, name="xin", align_bytes=64)
            words = dq[u][:].rearrange("p j f -> p (j f)").bitcast(F32)
            pt = psum.tile([P, 2, 2, P], F32, name="xt", tag="xt", bufs=CFG["xtb"])
            for a in range(2):
                jj = 2 * half + a
                for v in range(2):
                    nc.tensor.transpose(pt[:, a, v, :], words[:, jj * 256 + v : (jj + 1) * 256 : 2], ident[:])
            dst = xin[u][:, half * 1024 : (half + 1) * 1024].bitcast(F32)
            nc.scalar.copy(out=dst.rearrange("p (a r v) -> p a r v", a=2, v=2), in_=pt[:].rearrange("p a v r -> p a r v"))

        def interleave(out, in_, engine):
            if engine in "AV":
                dst = out.rearrange("p (c i) j -> p c j i", i=4)
                src = in_.rearrange("p (c i) j -> p c j i", i=4)
                if engine == "A":
                    nc.scalar.copy(out=dst, in_=src)
                else:
                    nc.vector.tensor_copy(out=dst, in_=src)
            else:
                nc.gpsimd.tensor_scalar(out=out, in0=in_, scalar1=1.0, scalar2=0.0, op0=ALU.mult, op1=ALU.add)

        def x1(u, a, engine):
            if a == 0:
                tin[u] = work.tile([P, 512, 4], BF16, name="tin", align_bytes=64)
            cols = slice(a * P, (a + 1) * P)
            interleave(tin[u][:, cols, :], dq[u][:, :, cols].rearrange("p j f -> p f j"), engine)

        def quant_f(u, half):
            G, h = ORD[u]
            w0, w1 = 256 * half, 256 * half + 256
            if CFG["qfm"] and u < 7:
                w0 = 0
                if half == 0:
                    return
            cols = slice(512 * h + w0, 512 * h + w1)
            nc.vector.quantize_mx(
                out=f_codes[G][:, cols].bitcast(E5M2), scales=f_scales[G][:, cols], in_=xin[u][:, 4 * w0 : 4 * w1]
            )

        def quant_t(u, a0, a1):
            if a0 == 0:
                t_codes[u] = work.tile([P, 512], U32, name="tcod", bufs=CFG["tb"], align_bytes=64)
                t_scales[u] = work.tile([P, 512], U8, name="tsca", bufs=CFG["tb"], align_bytes=64)
            cols = slice(a0 * P, a1 * P)
            nc.vector.quantize_mx(
                out=t_codes[u][:, cols].bitcast(E5M2), scales=t_scales[u][:, cols], in_=tin[u][:, cols, :].rearrange("p f j -> p (f j)")
            )

        mixed = {}
        MN = CFG["mixn"]

        def mix(key, n, engine):
            if CFG["qwm"] and MN == 256:
                if n % 2 == 0:
                    mixed[key, n // 2] = work.tile([P, 512, 4], BF16, name="mixed", align_bytes=64, bufs=CFG["mixb"])
                dst = mixed[key, n // 2][:, (n % 2) * 256 : (n % 2) * 256 + 256, :]
                interleave(dst, raw_tiles[key][:, :, n * MN : (n + 1) * MN].rearrange("p j c -> p c j"), engine)
                return
            t = work.tile([P, MN, 4], BF16, name="mixed", align_bytes=64, bufs=CFG["mixb"])
            if engine in "PQ":
                for c in range(MN // 256):
                    pt = psum.tile([P, 256, 4], BF16, name="pi", tag="mx", bufs=CFG["mxb"])
                    for j in range(4):
                        c0 = n * MN + c * 256
                        nc.tensor.matmul(pt[:, :, j], lhsT=identb[:], rhs=raw_tiles[key][:, j, c0 : c0 + 256], start=True, stop=True)
                    dst = t[:, c * 256 : (c + 1) * 256, :]
                    if engine == "P":
                        nc.scalar.copy(out=dst, in_=pt[:])
                    else:
                        nc.vector.tensor_copy(out=dst, in_=pt[:])
                mixed[key, n] = t
                return
            interleave(t[:], raw_tiles[key][:, :, n * MN : (n + 1) * MN].rearrange("p j c -> p c j"), engine)
            mixed[key, n] = t

        def quant_w(key, n):
            QN = MN
            if CFG["qwm"] and MN == 256:
                if n % 2 == 0:
                    return
                n, QN = n // 2, 512
            kind, i = key
            codes = (x_codes if kind == "x" else w_codes)[i]
            scales = (x_scales if kind == "x" else w_scales)[i]
            cols = slice(n * QN, (n + 1) * QN)
            nc.vector.quantize_mx(
                out=codes[:, cols].bitcast(E4M3), scales=scales[:, cols], in_=mixed[key, n][:].rearrange("p c j -> p (c j)")
            )

        stage = {}

        tags = [("mx", CFG["mxb"])]

        def mx_group(lhs, rhs, n, key, store, engine, add=None):
            tag, bufs = tags[0]
            tags.append(tags.pop(0))
            acc = psum.tile([P, 512], F32, name="acc", tag=tag, bufs=bufs)
            k = len(lhs)
            for i in range(k):
                (lc, ls, l0), (rc, rs) = lhs[i], rhs[i]
                nc.tensor.matmul_mx(
                    out=acc[:],
                    lhsT=lc[:, l0 : l0 + P].bitcast(E5M2),
                    lhsT_scale=ls[:, l0 : l0 + P],
                    rhs=rc[:, n * 512 : (n + 1) * 512].bitcast(E4M3),
                    rhs_scale=rs[:, n * 512 : (n + 1) * 512],
                    start=(i == 0),
                    stop=(i == k - 1),
                )
            if store is None:
                nc.scalar.copy(out=add, in_=acc[:])
                return
            if n == 0:
                stage[key] = work.tile([P, C], F32, name="ostage", bufs=CFG["ob"])
            dst = stage[key][:, n * 512 : (n + 1) * 512]
            if add is not None:
                nc.vector.tensor_tensor(out=dst, in0=acc[:], in1=add, op=ALU.add)
            elif engine == 0:
                nc.scalar.copy(out=dst, in_=acc[:])
            else:
                nc.vector.tensor_copy(out=dst, in_=acc[:])
            if n == 1:
                nc.sync.dma_start(out=store, in_=stage[key][:])

        def dw_group(G, a, n, engine=0):
            lhs = [(t_codes[ORD.index((G, h))], t_scales[ORD.index((G, h))], a * P) for h in range(2)]
            rhs = [(x_codes[h], x_scales[h]) for h in range(2)]
            r0 = (4 * G + a) * P
            mx_group(lhs, rhs, n, ("w", G, a), out_1[r0 : r0 + P, :], engine)

        def dx_group(h, jj, n, engine=0, Gs=range(NG), add=None, store=True):
            lhs = [(f_codes[G], f_scales[G], h * 512 + jj * P) for G in Gs]
            rhs = [(w_codes[G], w_scales[G]) for G in Gs]
            rows = of[512 * h : 512 * h + 512, :].rearrange("(p j) c -> p j c", j=4)
            mx_group(lhs, rhs, n, ("x", h, jj), rows[:, jj, :] if store else None, engine, add)

        part = const.tile([P, 4, C], F32, name="part") if CFG["part"] else None
        HL = ORD[7][1]
        GL = ORD[7][0]
        GP = [G for G in range(NG) if G != GL]
        load_at = {}
        for item in CFG["ls"].split():
            i, item = item.split(":")
            load_at.setdefault(int(i), []).append(int(item) if len(item) == 1 else (item[0], int(item[1])))
        keys = [(v[0], int(v[1])) for v in CFG["kx"]]
        mix_list = [(key, n) for key in keys for n in range(C // MN)]
        mix_at = {}
        msteps = [int(v) for v in CFG["mx"].split()]
        for k, item in enumerate(mix_list):
            mix_at.setdefault(msteps[k * MN // 512], []).append(item + (CFG["me"][k * MN // 512],))
        mx_queue = []
        df = CFG["fin"]
        stages = dict(t1=(0, t1), ab=(CFG["ab"], mul_ab), gc=(CFG["gc"], gcopy), bp=(CFG["bp"], mul_b), t2=(CFG["t2"], t2), d=(CFG["d"], mul_d), red=(CFG["red"], red), kq=(CFG["kq"], mul_kq), fin=(CFG["fin"], fin))
        if CFG["ts"]:
            table(ORD[0][1], 0, nc.vector, 0, 1)
            table(ORD[0][1], 1, nc.vector, 0, 1)
            t1(0)
            table(ORD[0][1], 0, nc.vector, 1, 4)
            table(ORD[0][1], 1, nc.vector, 1, 4)
        else:
            table(ORD[0][1], 0, nc.vector)
            t1(0)
            table(ORD[0][1], 1, nc.vector)
        if CFG["cu"] < 0:
            cube()
        step = 0
        while step < NS + df + 6 or mx_queue:
            i = step
            for item in load_at.get(i, []):
                if isinstance(item, int):
                    load(item)
                else:
                    src = xf if item[0] == "x" else wq
                    load_raw(item, src[512 * item[1] : 512 * item[1] + 512, :])
            for name in CFG["order"].split():
                off, fn = stages[name]
                if 0 <= i - off < NS and (name != "t1" or i > 0):
                    fn(i - off)
            if i == CFG["cu"]:
                cube()
            if i == CFG["tb1"]:
                table(1 - ORD[0][1], 0, nc.gpsimd)
                table(1 - ORD[0][1], 1, nc.gpsimd)
            for u in range(8):
                last = u == 7
                base = 4 * u + df
                for half in range(2):
                    ia = base + 2 * half + 1 + (CFG["lt"] if last else CFG["t3a"])
                    if i == ia:
                        t3(u, half)
                    if i == ia + (CFG["lq"] if last else CFG["qf"]):
                        quant_f(u, half)
                        h = ORD[u][1]
                        if CFG["qfm"] and u < 7 and half == 0:
                            pass
                        elif all(ORD.index((G, h)) <= u for G in range(NG)):
                            kind = "f" if CFG["part"] and h == HL else "x"
                            mx_queue += [(kind, h, jj, n) for jj in range(0 if CFG["qfm"] and u < 7 else 2 * half, 2 * half + 2) for n in range(2)]
                        elif CFG["part"] and h == HL and all(ORD.index((G, h)) <= u for G in GP):
                            mx_queue += [("p", h, jj, n) for jj in range(0 if CFG["qfm"] and u < 7 else 2 * half, 2 * half + 2) for n in range(2)]
                if not last:
                    per = CFG["x1per"]
                    for a in range(4):
                        if i == base + 4 + a // per:
                            x1(u, a, CFG["xe"][a])
                    if i == base + 4 + 4 // per:
                        quant_t(u, 0, 4)
                        G = ORD[u][0]
                        if all(ORD.index((G, h)) <= u for h in range(2)):
                            mx_queue += [("w", G, a, n) for a in range(4) for n in range(2)]
                elif i == base + 4:
                    for a in range(4):
                        x1(u, a, "VAGV"[a])
                    for a in range(4):
                        quant_t(u, a, a + 1)
                    mx_queue = [("w", ORD[u][0], a, n) for a in range(4) for n in range(2)] + mx_queue
            for item in mix_at.get(i, []):
                mix(*item)
            for item in mix_at.get(i - CFG["qw"], []):
                quant_w(*item[:2])
            tail = i > NS + df - 1
            if i == NS + df and CFG["tt"]:
                DH, GT, MX = ("dh", CFG["dhb"]), ("gT", CFG["gTb"]), ("mx", CFG["mxb"])
                tags[:] = [DH, GT, MX, DH, GT, MX, DH]
            left = 4 * CFG["tw"] if tail else (CFG["ebud"] if i >= NS else CFG["bud"])
            while mx_queue and left > 0:
                    kind, i0, i1, n = mx_queue.pop(0)
                    left -= {"w": 2, "x": 4, "p": 3, "f": 1}[kind]
                    engine = n if tail else 0
                    if kind == "w":
                        dw_group(i0, i1, n, engine)
                    elif kind == "x":
                        dx_group(i0, i1, n, engine)
                    else:
                        pc = part[:, i1, n * 512 : (n + 1) * 512]
                        dx_group(i0, i1, n, engine, GP if kind == "p" else [GL], pc, kind == "f")
            step += 1
